import numpy as np
import ml_dtypes


def mxq(x, axis, fmt="e4m3"):
    dtype, down = {"e4m3": (ml_dtypes.float8_e4m3fn, 7), "e5m2": (ml_dtypes.float8_e5m2, 14)}[fmt]
    v = np.moveaxis(np.asarray(x, np.float32).astype(ml_dtypes.bfloat16).astype(np.float64), axis, -1)
    blocks = v.reshape(v.shape[:-1] + (-1, 32))
    amax = np.abs(blocks).max(-1, keepdims=True)
    byte = np.maximum(np.where(amax > 0, np.frexp(amax)[1] - 1 + 127, 0) - down, 1)
    scale = np.exp2(byte - 127.0)
    codes = (blocks / scale).astype(np.float32).astype(dtype).astype(np.float64)
    return np.moveaxis((codes * scale).reshape(v.shape), -1, axis)


WIDE = False


def mx_kscale(k):
    if not WIDE:
        return np.ones(k)
    levels = np.array([10, -10, 5, -5, 0])
    a = np.random.permutation(np.resize(levels, k // 512 * 4)).reshape(k // 512, 4)
    idx = np.arange(k)
    return np.exp2(a[idx // 512, idx % 128 // 32])


BF16 = ml_dtypes.bfloat16


def bf(x):
    return np.asarray(x, np.float32).astype(BF16)


def f64(x):
    return np.asarray(x).astype(np.float64)


B, N, D, H = 2, 2048, 512, 512
EDGE_P = 0.01
DEG = 1.0 + EDGE_P * N


def normalize_adj(adj):
    rowsum = adj.sum(axis=1)
    d_inv_sqrt = np.where(rowsum > 0, 1.0 / np.sqrt(np.maximum(rowsum, 1e-30)), 0.0)
    return d_inv_sqrt[:, :, None] * adj.transpose(0, 2, 1) * d_inv_sqrt[:, None, :]


def setup_inputs():
    t = mx_kscale(H)
    adj = (np.random.uniform(size=(B, N, N)) < EDGE_P).astype(np.float64)
    adj = np.minimum(adj + np.eye(N)[None], 1.0)
    return {"msg": bf(np.random.standard_normal((B, N, H)) * 0.5 * np.sqrt(DEG) * t),
            "adj": bf(adj),
            "b2": bf(np.random.standard_normal(H) * 0.2 * t),
            "W3": bf(np.random.standard_normal((H, D)) * 0.5 * np.sqrt(DEG / H) / t[:, None])}


def reference(msg, adj, b2, W3):
    a = normalize_adj(f64(adj))
    h = np.maximum((mxq(a, 2, "e4m3") @ mxq(f64(msg), 1, "e4m3")) + f64(b2), 0.0)
    return mxq(h, 2, "e4m3") @ mxq(f64(W3), 0, "e4m3")

@@ -1,0 +1,356 @@
+from contextlib import ExitStack
+
+import concourse.mybir as mybir
+from concourse.masks import make_identity
+
+F32 = mybir.dt.float32
+BF16 = mybir.dt.bfloat16
+U32 = mybir.dt.uint32
+U8 = mybir.dt.uint8
+FP8X4 = mybir.dt.float8_e4m3fn_x4
+ALU = mybir.AluOpType
+ACT = mybir.ActivationFunctionType
+AXIS = mybir.AxisListType
+
+BATCH, NODES, HIDDEN, OUT_DIM = 2, 2048, 512, 512
+FLOPS = 2 * BATCH * NODES * NODES * HIDDEN + 2 * BATCH * NODES * HIDDEN * OUT_DIM
+
+P = 128
+PACK = 4
+K_PASS = P * PACK
+PASSES = NODES // K_PASS
+ROW_BLOCKS = NODES // P
+HALF = NODES // 2
+BLOCKS_PER_HALF = HALF // P
+PASSES_PER_HALF = HALF // K_PASS
+CHUNK = 512
+CHUNKS = NODES // CHUNK
+CHUNKS_PER_HALF = HALF // CHUNK
+BLOCKS_PER_CHUNK = CHUNK // P
+F_TILES = HIDDEN // P
+RUN = 4
+ADJ_BUFS = 3
+RAW_BUFS = 6
+
+UNITS_PER_BATCH = CHUNKS * PASSES
+EARLY_UNITS = CHUNKS_PER_HALF * PASSES_PER_HALF
+FIRST_HALF_UNITS = CHUNKS_PER_HALF * PASSES
+
+assert HIDDEN == K_PASS and HIDDEN == CHUNK and OUT_DIM == CHUNK and F_TILES == PACK
+
+
+def tile_perception_pb_kernel(tc, msg, adj, b2, W3, out):
+    nc = tc.nc
+    with ExitStack() as ctx:
+        keep = ctx.enter_context(tc.tile_pool(name="keep", bufs=1))
+        adj_pool = ctx.enter_context(tc.tile_pool(name="adj_pool", bufs=ADJ_BUFS))
+        raw_pool = ctx.enter_context(tc.tile_pool(name="raw_pool", bufs=RAW_BUFS))
+        work = ctx.enter_context(tc.tile_pool(name="work", bufs=4))
+        codes_pool = ctx.enter_context(tc.tile_pool(name="codes_pool", bufs=2))
+        small = ctx.enter_context(tc.tile_pool(name="small", bufs=2))
+        degree_pool = ctx.enter_context(tc.tile_pool(name="degree_pool", bufs=BATCH * 2))
+        out_pool = ctx.enter_context(tc.tile_pool(name="out_pool", bufs=4))
+        psum_acc = ctx.enter_context(tc.psum_pool(name="psum_acc", bufs=F_TILES))
+        psum_out = ctx.enter_context(tc.psum_pool(name="psum_out", bufs=2))
+        psum_aux = ctx.enter_context(tc.psum_pool(name="psum_aux", bufs=2))
+        ctx.enter_context(tc.manual_schedule())
+
+        def regroup(copy, planes):
+            grouped = work.tile([P, CHUNK, PACK], BF16, name="grouped", tag="grouped", align_bytes=64)
+            copy(
+                out=grouped.rearrange("p (c i) t -> p c t i", i=RUN),
+                in_=planes.rearrange("p t (c i) -> p c t i", i=RUN),
+            )
+            return grouped
+
+        def quantise(grouped, codes, scales):
+            nc.vector.quantize_mx(
+                out=codes.bitcast(FP8X4),
+                scales=scales,
+                in_=grouped.rearrange("p w t -> p (w t)"),
+            )
+
+        warm = keep.tile([P, 1], F32, name="warm")
+        nc.vector.memset(warm[:], 1.0)
+        nc.scalar.activation(out=warm[:], in_=warm[:], func=ACT.Sqrt)
+        ident = keep.tile([P, P], F32, name="ident")
+        make_identity(nc, ident[:])
+        ones = keep.tile([P, 1], BF16, name="ones")
+        nc.vector.memset(ones[:], 1.0)
+
+        b2_rows = keep.tile([P, P], BF16, name="b2_rows")
+        nc.vector.memset(b2_rows[:], 0.0)
+        nc.sync.dma_start(out=b2_rows[0:PACK, :], in_=b2.rearrange("(t p) -> t p", p=P))
+        b2_rows_f32 = keep.tile([P, P], F32, name="b2_rows_f32")
+        nc.vector.tensor_copy(out=b2_rows_f32[:], in_=b2_rows[:])
+        b2_ps = psum_aux.tile([P, P], F32, name="b2_ps", tag="aux")
+        nc.tensor.transpose(out=b2_ps[:], in_=b2_rows_f32[:], identity=ident[:])
+        b2_col = keep.tile([P, PACK], F32, name="b2_col")
+        nc.vector.tensor_copy(out=b2_col[:], in_=b2_ps[:, 0:PACK])
+
+        msg_codes = keep.tile([P, BATCH, PASSES, HIDDEN], U32, name="msg_codes", align_bytes=64)
+        msg_scales = keep.tile([P, BATCH, PASSES, HIDDEN], U8, name="msg_scales", align_bytes=64)
+        w3_codes = keep.tile([P, OUT_DIM], U32, name="w3_codes", align_bytes=64)
+        w3_scales = keep.tile([P, OUT_DIM], U8, name="w3_scales", align_bytes=64)
+        pieces = []
+        for b in range(BATCH):
+            rows = msg[b].rearrange("(g t p) f -> g p t f", t=PACK, p=P)
+            for g in range(PASSES):
+                pieces.append((rows[g], msg_codes[:, b, g, :], msg_scales[:, b, g, :]))
+        pieces.append((W3.rearrange("(t p) d -> p t d", p=P), w3_codes[:], w3_scales[:]))
+        raws = {}
+        piece_grouped = {}
+        for n in range(len(pieces) + RAW_BUFS + 1):
+            if 0 <= n - RAW_BUFS - 1:
+                quantise(piece_grouped[n - RAW_BUFS - 1], pieces[n - RAW_BUFS - 1][1], pieces[n - RAW_BUFS - 1][2])
+            if 0 <= n - RAW_BUFS < len(pieces):
+                copy = nc.vector.tensor_copy if n % 2 == 0 else nc.scalar.copy
+                piece_grouped[n - RAW_BUFS] = regroup(copy, raws[n - RAW_BUFS])
+            if n < len(pieces):
+                raws[n] = raw_pool.tile([P, PACK, CHUNK], BF16, name="raw", tag="raw")
+                nc.sync.dma_start(out=raws[n][:], in_=pieces[n][0])
+
+        adj_halves = {}
+
+        def load_half(b, hf):
+            half = adj_pool.tile([P, ROW_BLOCKS, HALF], BF16, name="half", tag="half")
+            rows = adj[b].rearrange("(k p) i -> p k i", p=P)
+            for g in range(PASSES):
+                blocks = slice(g * PACK, (g + 1) * PACK)
+                nc.sync.dma_start(out=half[:, blocks, :], in_=rows[:, blocks, hf * HALF : (hf + 1) * HALF])
+            adj_halves[(b, hf)] = half
+
+        sums = {}
+        c_floor = {}
+        root = {}
+        positive = {}
+        d_col = {}
+        d_row = {}
+        half_shape = [P, BLOCKS_PER_HALF]
+
+        def column_sums(b, hf, g):
+            if g == 0:
+                sums[(b, hf)] = psum_aux.tile([P, BLOCKS_PER_HALF, PASSES], F32, name="sums", tag="aux")
+            for blk in range(BLOCKS_PER_HALF):
+                for t in range(PACK):
+                    nc.tensor.matmul(
+                        out=sums[(b, hf)][:, blk, g : g + 1],
+                        lhsT=adj_halves[(b, hf)][:, g * PACK + t, blk * P : (blk + 1) * P],
+                        rhs=ones[:],
+                        start=(t == 0),
+                        stop=(t == PACK - 1),
+                    )
+
+        def degrees_begin(b, hf):
+            c = small.tile(half_shape, F32, name="c", tag="c")
+            nc.vector.tensor_reduce(out=c[:], in_=sums[(b, hf)][:], axis=AXIS.X, op=ALU.add)
+            c_floor[(b, hf)] = small.tile(half_shape, F32, name="c_floor", tag="c_floor")
+            nc.vector.tensor_scalar_max(out=c_floor[(b, hf)][:], in0=c[:], scalar1=1e-30)
+            root[(b, hf)] = small.tile(half_shape, F32, name="root", tag="root")
+            nc.scalar.activation(out=root[(b, hf)][:], in_=c_floor[(b, hf)][:], func=ACT.Sqrt)
+            positive[(b, hf)] = small.tile(half_shape, F32, name="positive", tag="positive")
+            nc.vector.tensor_single_scalar(out=positive[(b, hf)][:], in_=c[:], scalar=0.0, op=ALU.is_gt)
+
+        def degrees_end(b, hf):
+            guess = small.tile(half_shape, F32, name="guess", tag="guess")
+            nc.vector.reciprocal(out=guess[:], in_=root[(b, hf)][:])
+            square = small.tile(half_shape, F32, name="square", tag="square")
+            nc.vector.tensor_mul(out=square[:], in0=guess[:], in1=guess[:])
+            masked = small.tile(half_shape, F32, name="masked", tag="masked")
+            nc.vector.tensor_mul(out=masked[:], in0=guess[:], in1=positive[(b, hf)][:])
+            step = small.tile(half_shape, F32, name="step", tag="step")
+            nc.vector.scalar_tensor_tensor(
+                out=step[:], in0=square[:], scalar=-0.5, in1=c_floor[(b, hf)][:], op0=ALU.mult, op1=ALU.mult
+            )
+            d = degree_pool.tile(half_shape, F32, name="d", tag="d")
+            nc.vector.scalar_tensor_tensor(
+                out=d[:], in0=step[:], scalar=1.5, in1=masked[:], op0=ALU.add, op1=ALU.mult
+            )
+            d_col[(b, hf)] = d
+
+        def spread_rows(b, hf):
+            d_row[(b, hf)] = degree_pool.tile([P, HALF], F32, name="row", tag="row")
+            for q in range(CHUNKS_PER_HALF):
+                spread_ps = psum_aux.tile([P, CHUNK], F32, name="spread_ps", tag="aux")
+                for k in range(BLOCKS_PER_CHUNK):
+                    blk = q * BLOCKS_PER_CHUNK + k
+                    nc.tensor.transpose(
+                        out=spread_ps[:, k * P : (k + 1) * P],
+                        in_=d_col[(b, hf)][:, blk : blk + 1].to_broadcast([P, P]),
+                        identity=ident[:],
+                    )
+                nc.scalar.copy(out=d_row[(b, hf)][:, q * CHUNK : (q + 1) * CHUNK], in_=spread_ps[:])
+
+        units = []
+        for b in range(BATCH):
+            for chunk in range(CHUNKS_PER_HALF):
+                for g in range(PASSES_PER_HALF):
+                    units.append((b, chunk, g))
+            for chunk in range(CHUNKS):
+                for g in range(PASSES):
+                    if chunk >= CHUNKS_PER_HALF or g >= PASSES_PER_HALF:
+                        units.append((b, chunk, g))
+
+        a_planes = {}
+        a_grouped = {}
+        a_codes = {}
+        a_scales = {}
+        acc = {}
+        h_planes = {}
+        h_grouped = {}
+        h_codes = {}
+        h_scales = {}
+        o_ps = {}
+
+        def scale(b, chunk, g):
+            hf_cols, first_col = divmod(chunk * CHUNK, HALF)
+            cols = slice(first_col, first_col + CHUNK)
+            planes = work.tile([P, PACK, CHUNK], BF16, name="planes", tag="planes")
+            for t in range(PACK):
+                hf_rows, blk = divmod(g * PACK + t, BLOCKS_PER_HALF)
+                nc.vector.scalar_tensor_tensor(
+                    out=planes[:, t, :],
+                    in0=adj_halves[(b, hf_cols)][:, g * PACK + t, cols],
+                    scalar=d_col[(b, hf_rows)][:, blk : blk + 1],
+                    in1=d_row[(b, hf_cols)][:, cols],
+                    op0=ALU.mult,
+                    op1=ALU.mult,
+                )
+            a_planes[(b, chunk, g)] = planes
+
+        def regroup_a(b, chunk, g):
+            a_grouped[(b, chunk, g)] = regroup(nc.scalar.copy, a_planes[(b, chunk, g)])
+
+        def quantise_a(b, chunk, g):
+            if g == 0:
+                a_codes[(b, chunk)] = codes_pool.tile(
+                    [P, PASSES, CHUNK], U32, name="a_codes", tag="a_codes", align_bytes=64
+                )
+                a_scales[(b, chunk)] = codes_pool.tile(
+                    [P, PASSES, CHUNK], U8, name="a_scales", tag="a_scales", align_bytes=64
+                )
+            quantise(a_grouped[(b, chunk, g)], a_codes[(b, chunk)][:, g, :], a_scales[(b, chunk)][:, g, :])
+
+        def aggregate(b, chunk, g):
+            if chunk < CHUNKS_PER_HALF and g < PASSES_PER_HALF:
+                return
+            first = 0 if (chunk < CHUNKS_PER_HALF and g == PASSES_PER_HALF) else g
+            if first == 0:
+                acc[(b, chunk)] = [
+                    psum_acc.tile([P, CHUNK], F32, name="acc%d" % ft, tag="acc") for ft in range(F_TILES)
+                ]
+            for gg in range(first, g + 1):
+                for ft in range(F_TILES):
+                    f_cols = slice(ft * P, (ft + 1) * P)
+                    nc.tensor.matmul_mx(
+                        out=acc[(b, chunk)][ft][:],
+                        lhsT=msg_codes[:, b, gg, f_cols].bitcast(FP8X4),
+                        lhsT_scale=msg_scales[:, b, gg, f_cols],
+                        rhs=a_codes[(b, chunk)][:, gg, :].bitcast(FP8X4),
+                        rhs_scale=a_scales[(b, chunk)][:, gg, :],
+                        start=(gg == 0),
+                        stop=(gg == PASSES - 1),
+                    )
+
+        def relu(b, chunk):
+            h_planes[(b, chunk)] = work.tile([P, PACK, CHUNK], BF16, name="h_planes", tag="planes")
+            for ft in range(F_TILES):
+                nc.scalar.activation(
+                    out=h_planes[(b, chunk)][:, ft, :],
+                    in_=acc[(b, chunk)][ft][:],
+                    func=ACT.Relu,
+                    bias=b2_col[:, ft : ft + 1],
+                    scale=1.0,
+                )
+
+        def regroup_h(b, chunk):
+            h_grouped[(b, chunk)] = regroup(nc.vector.tensor_copy, h_planes[(b, chunk)])
+
+        def quantise_h(b, chunk):
+            h_codes[(b, chunk)] = codes_pool.tile([P, CHUNK], U32, name="h_codes", tag="h_codes", align_bytes=64)
+            h_scales[(b, chunk)] = codes_pool.tile([P, CHUNK], U8, name="h_scales", tag="h_scales", align_bytes=64)
+            quantise(h_grouped[(b, chunk)], h_codes[(b, chunk)][:], h_scales[(b, chunk)][:])
+
+        def project(b, chunk):
+            for it in range(BLOCKS_PER_CHUNK):
+                i_cols = slice(it * P, (it + 1) * P)
+                o_ps[(b, chunk, it)] = psum_out.tile([P, OUT_DIM], F32, name="o_ps", tag="o_ps")
+                nc.tensor.matmul_mx(
+                    out=o_ps[(b, chunk, it)][:],
+                    lhsT=h_codes[(b, chunk)][:, i_cols].bitcast(FP8X4),
+                    lhsT_scale=h_scales[(b, chunk)][:, i_cols],
+                    rhs=w3_codes[:].bitcast(FP8X4),
+                    rhs_scale=w3_scales[:],
+                    start=True,
+                    stop=True,
+                )
+
+        def store(b, chunk):
+            for it in range(BLOCKS_PER_CHUNK):
+                o_sb = out_pool.tile([P, OUT_DIM], F32, name="o_sb", tag="o_sb")
+                nc.scalar.copy(out=o_sb[:], in_=o_ps[(b, chunk, it)][:])
+                first_row = chunk * CHUNK + it * P
+                nc.sync.dma_start(out=out[b, first_row : first_row + P, :], in_=o_sb[:])
+
+        load_half(0, 0)
+        load_half(0, 1)
+        load_half(1, 0)
+        for g in range(PASSES):
+            column_sums(0, 0, g)
+        degrees_begin(0, 0)
+        degrees_end(0, 0)
+        spread_rows(0, 0)
+        for g in range(PASSES):
+            column_sums(0, 1, g)
+
+        def prepare(step):
+            b, local = divmod(step, UNITS_PER_BATCH)
+            if b >= BATCH:
+                return
+            if b == 0 and local == EARLY_UNITS:
+                degrees_begin(0, 1)
+                degrees_end(0, 1)
+                spread_rows(0, 1)
+            if b > 0 and local == 0:
+                degrees_begin(b, 1)
+            if b > 0 and local == 2:
+                degrees_end(b, 1)
+                spread_rows(b, 1)
+            if b + 1 < BATCH:
+                if local == FIRST_HALF_UNITS:
+                    load_half(b + 1, 1)
+                if FIRST_HALF_UNITS <= local < FIRST_HALF_UNITS + PASSES:
+                    column_sums(b + 1, 0, local - FIRST_HALF_UNITS)
+                if local == FIRST_HALF_UNITS + PASSES:
+                    degrees_begin(b + 1, 0)
+                if FIRST_HALF_UNITS + PASSES <= local:
+                    column_sums(b + 1, 1, local - FIRST_HALF_UNITS - PASSES)
+                if local == FIRST_HALF_UNITS + PASSES + 2:
+                    degrees_end(b + 1, 0)
+                    spread_rows(b + 1, 0)
+
+        def unit_at(step, lag):
+            return units[step - lag] if 0 <= step - lag < len(units) else None
+
+        def closing_at(step, lag):
+            unit = unit_at(step, lag)
+            return unit[0:2] if unit is not None and unit[2] == PASSES - 1 else None
+
+        for step in range(len(units) + 6):
+            prepare(step)
+            if unit_at(step, 0) is not None:
+                scale(*unit_at(step, 0))
+            if unit_at(step, 1) is not None:
+                regroup_a(*unit_at(step, 1))
+            if closing_at(step, 4) is not None:
+                regroup_h(*closing_at(step, 4))
+            if unit_at(step, 2) is not None:
+                quantise_a(*unit_at(step, 2))
+                aggregate(*unit_at(step, 2))
+            if closing_at(step, 3) is not None:
+                relu(*closing_at(step, 3))
+            if closing_at(step, 4) is not None:
+                quantise_h(*closing_at(step, 4))
+                project(*closing_at(step, 4))
+            if closing_at(step, 5) is not None:
+                store(*closing_at(step, 5))

@@ -53,7 +53,6 @@ def tile_perception_pb_kernel(tc, msg, adj, b2, W3, out):
         psum_acc = ctx.enter_context(tc.psum_pool(name="psum_acc", bufs=F_TILES))
         psum_out = ctx.enter_context(tc.psum_pool(name="psum_out", bufs=2))
         psum_aux = ctx.enter_context(tc.psum_pool(name="psum_aux", bufs=2))
-        ctx.enter_context(tc.manual_schedule())
 
         def regroup(copy, planes):
             grouped = work.tile([P, CHUNK, PACK], BF16, name="grouped", tag="grouped", align_bytes=64)

@@ -45,7 +45,7 @@ def tile_perception_pb_kernel(tc, msg, adj, b2, W3, out):
         keep = ctx.enter_context(tc.tile_pool(name="keep", bufs=1))
         adj_pool = ctx.enter_context(tc.tile_pool(name="adj_pool", bufs=ADJ_BUFS))
         raw_pool = ctx.enter_context(tc.tile_pool(name="raw_pool", bufs=RAW_BUFS))
-        work = ctx.enter_context(tc.tile_pool(name="work", bufs=4))
+        work = ctx.enter_context(tc.tile_pool(name="work", bufs=5))
         codes_pool = ctx.enter_context(tc.tile_pool(name="codes_pool", bufs=2))
         small = ctx.enter_context(tc.tile_pool(name="small", bufs=2))
         degree_pool = ctx.enter_context(tc.tile_pool(name="degree_pool", bufs=BATCH * 2))
@@ -178,7 +178,8 @@ def tile_perception_pb_kernel(tc, msg, adj, b2, W3, out):
                         in_=d_col[(b, hf)][:, blk : blk + 1].to_broadcast([P, P]),
                         identity=ident[:],
                     )
-                nc.scalar.copy(out=d_row[(b, hf)][:, q * CHUNK : (q + 1) * CHUNK], in_=spread_ps[:])
+                copy = nc.vector.tensor_copy if q % 2 == 0 else nc.scalar.copy
+                copy(out=d_row[(b, hf)][:, q * CHUNK : (q + 1) * CHUNK], in_=spread_ps[:])
 
         units = []
         for b in range(BATCH):
@@ -217,8 +218,13 @@ def tile_perception_pb_kernel(tc, msg, adj, b2, W3, out):
                 )
             a_planes[(b, chunk, g)] = planes
 
+        def is_last_chunk(b, chunk):
+            return (b, chunk) == (BATCH - 1, CHUNKS - 1)
+
         def regroup_a(b, chunk, g):
-            a_grouped[(b, chunk, g)] = regroup(nc.scalar.copy, a_planes[(b, chunk, g)])
+            last_unit = is_last_chunk(b, chunk) and g == PASSES - 1
+            copy = nc.vector.tensor_copy if last_unit else nc.scalar.copy
+            a_grouped[(b, chunk, g)] = regroup(copy, a_planes[(b, chunk, g)])
 
         def quantise_a(b, chunk, g):
             if g == 0:
@@ -254,13 +260,23 @@ def tile_perception_pb_kernel(tc, msg, adj, b2, W3, out):
         def relu(b, chunk):
             h_planes[(b, chunk)] = work.tile([P, PACK, CHUNK], BF16, name="h_planes", tag="planes")
             for ft in range(F_TILES):
-                nc.scalar.activation(
-                    out=h_planes[(b, chunk)][:, ft, :],
-                    in_=acc[(b, chunk)][ft][:],
-                    func=ACT.Relu,
-                    bias=b2_col[:, ft : ft + 1],
-                    scale=1.0,
-                )
+                if is_last_chunk(b, chunk) and ft % 2 == 1:
+                    nc.vector.tensor_scalar(
+                        out=h_planes[(b, chunk)][:, ft, :],
+                        in0=acc[(b, chunk)][ft][:],
+                        scalar1=b2_col[:, ft : ft + 1],
+                        scalar2=0.0,
+                        op0=ALU.add,
+                        op1=ALU.max,
+                    )
+                else:
+                    nc.scalar.activation(
+                        out=h_planes[(b, chunk)][:, ft, :],
+                        in_=acc[(b, chunk)][ft][:],
+                        func=ACT.Relu,
+                        bias=b2_col[:, ft : ft + 1],
+                        scale=1.0,
+                    )
 
         def regroup_h(b, chunk):
             h_grouped[(b, chunk)] = regroup(nc.vector.tensor_copy, h_planes[(b, chunk)])
@@ -287,7 +303,8 @@ def tile_perception_pb_kernel(tc, msg, adj, b2, W3, out):
         def store(b, chunk):
             for it in range(BLOCKS_PER_CHUNK):
                 o_sb = out_pool.tile([P, OUT_DIM], F32, name="o_sb", tag="o_sb")
-                nc.scalar.copy(out=o_sb[:], in_=o_ps[(b, chunk, it)][:])
+                copy = nc.vector.tensor_copy if is_last_chunk(b, chunk) and it % 2 == 1 else nc.scalar.copy
+                copy(out=o_sb[:], in_=o_ps[(b, chunk, it)][:])
                 first_row = chunk * CHUNK + it * P
                 nc.sync.dma_start(out=out[b, first_row : first_row + P, :], in_=o_sb[:])
 
@@ -335,21 +352,21 @@ def tile_perception_pb_kernel(tc, msg, adj, b2, W3, out):
             unit = unit_at(step, lag)
             return unit[0:2] if unit is not None and unit[2] == PASSES - 1 else None
 
-        for step in range(len(units) + 6):
+        for step in range(len(units) + 7):
             prepare(step)
             if unit_at(step, 0) is not None:
                 scale(*unit_at(step, 0))
             if unit_at(step, 1) is not None:
                 regroup_a(*unit_at(step, 1))
-            if closing_at(step, 4) is not None:
-                regroup_h(*closing_at(step, 4))
-            if unit_at(step, 2) is not None:
-                quantise_a(*unit_at(step, 2))
-                aggregate(*unit_at(step, 2))
-            if closing_at(step, 3) is not None:
-                relu(*closing_at(step, 3))
-            if closing_at(step, 4) is not None:
-                quantise_h(*closing_at(step, 4))
-                project(*closing_at(step, 4))
             if closing_at(step, 5) is not None:
-                store(*closing_at(step, 5))
+                regroup_h(*closing_at(step, 5))
+            if unit_at(step, 3) is not None:
+                quantise_a(*unit_at(step, 3))
+                aggregate(*unit_at(step, 3))
+            if closing_at(step, 4) is not None:
+                relu(*closing_at(step, 4))
+            if closing_at(step, 5) is not None:
+                quantise_h(*closing_at(step, 5))
+                project(*closing_at(step, 5))
+            if closing_at(step, 6) is not None:
+                store(*closing_at(step, 6))

@@ -21,6 +21,7 @@ K_PASS = P * PACK
 PASSES = NODES // K_PASS
 ROW_BLOCKS = NODES // P
 HALF = NODES // 2
+HALVES = NODES // HALF
 BLOCKS_PER_HALF = HALF // P
 PASSES_PER_HALF = HALF // K_PASS
 CHUNK = 512
@@ -29,8 +30,18 @@ CHUNKS_PER_HALF = HALF // CHUNK
 BLOCKS_PER_CHUNK = CHUNK // P
 F_TILES = HIDDEN // P
 RUN = 4
+
 ADJ_BUFS = 3
+LOAD_BLOCKS = 2
 RAW_BUFS = 6
+WORK_BUFS = 5
+
+LAG_REGROUP = 1
+LAG_QUANTISE = LAG_REGROUP + 2
+LAG_RELU = LAG_QUANTISE + 1
+LAG_REQUANTISE = LAG_RELU + 1
+LAG_STORE = LAG_REQUANTISE + 1
+DEGREE_GAP = 2
 
 UNITS_PER_BATCH = CHUNKS * PASSES
 EARLY_UNITS = CHUNKS_PER_HALF * PASSES_PER_HALF
@@ -45,11 +56,11 @@ def tile_perception_pb_kernel(tc, msg, adj, b2, W3, out):
         keep = ctx.enter_context(tc.tile_pool(name="keep", bufs=1))
         adj_pool = ctx.enter_context(tc.tile_pool(name="adj_pool", bufs=ADJ_BUFS))
         raw_pool = ctx.enter_context(tc.tile_pool(name="raw_pool", bufs=RAW_BUFS))
-        work = ctx.enter_context(tc.tile_pool(name="work", bufs=5))
+        work = ctx.enter_context(tc.tile_pool(name="work", bufs=WORK_BUFS))
         codes_pool = ctx.enter_context(tc.tile_pool(name="codes_pool", bufs=2))
         small = ctx.enter_context(tc.tile_pool(name="small", bufs=2))
-        degree_pool = ctx.enter_context(tc.tile_pool(name="degree_pool", bufs=BATCH * 2))
-        out_pool = ctx.enter_context(tc.tile_pool(name="out_pool", bufs=4))
+        degree_pool = ctx.enter_context(tc.tile_pool(name="degree_pool", bufs=BATCH * HALVES))
+        out_pool = ctx.enter_context(tc.tile_pool(name="out_pool", bufs=BLOCKS_PER_CHUNK))
         psum_acc = ctx.enter_context(tc.psum_pool(name="psum_acc", bufs=F_TILES))
         psum_out = ctx.enter_context(tc.psum_pool(name="psum_out", bufs=2))
         psum_aux = ctx.enter_context(tc.psum_pool(name="psum_aux", bufs=2))
@@ -77,6 +88,77 @@ def tile_perception_pb_kernel(tc, msg, adj, b2, W3, out):
         ones = keep.tile([P, 1], BF16, name="ones")
         nc.vector.memset(ones[:], 1.0)
 
+        adj_halves = {}
+        sums = {}
+        c_floor = {}
+        root = {}
+        positive = {}
+        d_col = {}
+        d_row = {}
+        half_shape = [P, BLOCKS_PER_HALF]
+
+        def load_half(b, hf):
+            half = adj_pool.tile([P, ROW_BLOCKS, HALF], BF16, name="half", tag="half")
+            rows = adj[b].rearrange("(k p) i -> p k i", p=P)
+            for first in range(0, ROW_BLOCKS, LOAD_BLOCKS):
+                blocks = slice(first, first + LOAD_BLOCKS)
+                nc.sync.dma_start(out=half[:, blocks, :], in_=rows[:, blocks, hf * HALF : (hf + 1) * HALF])
+            adj_halves[(b, hf)] = half
+
+        def column_sums(b, hf):
+            sums[(b, hf)] = psum_aux.tile([P, BLOCKS_PER_HALF, ROW_BLOCKS], F32, name="sums", tag="aux")
+            for k in range(ROW_BLOCKS):
+                for blk in range(BLOCKS_PER_HALF):
+                    nc.tensor.matmul(
+                        out=sums[(b, hf)][:, blk, k : k + 1],
+                        lhsT=adj_halves[(b, hf)][:, k, blk * P : (blk + 1) * P],
+                        rhs=ones[:],
+                        start=True,
+                        stop=True,
+                    )
+
+        def degrees_begin(b, hf):
+            c = small.tile(half_shape, F32, name="c", tag="c")
+            nc.vector.tensor_reduce(out=c[:], in_=sums[(b, hf)][:], axis=AXIS.X, op=ALU.add)
+            c_floor[(b, hf)] = small.tile(half_shape, F32, name="c_floor", tag="c_floor")
+            nc.vector.tensor_scalar_max(out=c_floor[(b, hf)][:], in0=c[:], scalar1=1e-30)
+            root[(b, hf)] = small.tile(half_shape, F32, name="root", tag="root")
+            nc.scalar.activation(out=root[(b, hf)][:], in_=c_floor[(b, hf)][:], func=ACT.Sqrt)
+            positive[(b, hf)] = small.tile(half_shape, F32, name="positive", tag="positive")
+            nc.vector.tensor_single_scalar(out=positive[(b, hf)][:], in_=c[:], scalar=0.0, op=ALU.is_gt)
+
+        def degrees_end(b, hf):
+            guess = small.tile(half_shape, F32, name="guess", tag="guess")
+            nc.vector.reciprocal(out=guess[:], in_=root[(b, hf)][:])
+            square = small.tile(half_shape, F32, name="square", tag="square")
+            nc.vector.tensor_mul(out=square[:], in0=guess[:], in1=guess[:])
+            masked = small.tile(half_shape, F32, name="masked", tag="masked")
+            nc.vector.tensor_mul(out=masked[:], in0=guess[:], in1=positive[(b, hf)][:])
+            step = small.tile(half_shape, F32, name="step", tag="step")
+            nc.vector.scalar_tensor_tensor(
+                out=step[:], in0=square[:], scalar=-0.5, in1=c_floor[(b, hf)][:], op0=ALU.mult, op1=ALU.mult
+            )
+            d_col[(b, hf)] = degree_pool.tile(half_shape, F32, name="d", tag="d")
+            nc.vector.scalar_tensor_tensor(
+                out=d_col[(b, hf)][:], in0=step[:], scalar=1.5, in1=masked[:], op0=ALU.add, op1=ALU.mult
+            )
+            d_row[(b, hf)] = degree_pool.tile([P, HALF], F32, name="row", tag="row")
+            for q in range(CHUNKS_PER_HALF):
+                spread_ps = psum_aux.tile([P, CHUNK], F32, name="spread_ps", tag="aux")
+                for n in range(BLOCKS_PER_CHUNK):
+                    blk = q * BLOCKS_PER_CHUNK + n
+                    nc.tensor.transpose(
+                        out=spread_ps[:, n * P : (n + 1) * P],
+                        in_=d_col[(b, hf)][:, blk : blk + 1].to_broadcast([P, P]),
+                        identity=ident[:],
+                    )
+                nc.scalar.copy(out=d_row[(b, hf)][:, q * CHUNK : (q + 1) * CHUNK], in_=spread_ps[:])
+
+        load_half(0, 0)
+        column_sums(0, 0)
+        degrees_begin(0, 0)
+        degrees_end(0, 0)
+
         b2_rows = keep.tile([P, P], BF16, name="b2_rows")
         nc.vector.memset(b2_rows[:], 0.0)
         nc.sync.dma_start(out=b2_rows[0:PACK, :], in_=b2.rearrange("(t p) -> t p", p=P))
@@ -101,85 +183,19 @@ def tile_perception_pb_kernel(tc, msg, adj, b2, W3, out):
         piece_grouped = {}
         for n in range(len(pieces) + RAW_BUFS + 1):
             if 0 <= n - RAW_BUFS - 1:
-                quantise(piece_grouped[n - RAW_BUFS - 1], pieces[n - RAW_BUFS - 1][1], pieces[n - RAW_BUFS - 1][2])
+                source, codes, scales = pieces[n - RAW_BUFS - 1]
+                quantise(piece_grouped[n - RAW_BUFS - 1], codes, scales)
             if 0 <= n - RAW_BUFS < len(pieces):
                 copy = nc.vector.tensor_copy if n % 2 == 0 else nc.scalar.copy
                 piece_grouped[n - RAW_BUFS] = regroup(copy, raws[n - RAW_BUFS])
             if n < len(pieces):
+                source, codes, scales = pieces[n]
                 raws[n] = raw_pool.tile([P, PACK, CHUNK], BF16, name="raw", tag="raw")
-                nc.sync.dma_start(out=raws[n][:], in_=pieces[n][0])
+                nc.sync.dma_start(out=raws[n][:], in_=source)
 
-        adj_halves = {}
-
-        def load_half(b, hf):
-            half = adj_pool.tile([P, ROW_BLOCKS, HALF], BF16, name="half", tag="half")
-            rows = adj[b].rearrange("(k p) i -> p k i", p=P)
-            for g in range(PASSES):
-                blocks = slice(g * PACK, (g + 1) * PACK)
-                nc.sync.dma_start(out=half[:, blocks, :], in_=rows[:, blocks, hf * HALF : (hf + 1) * HALF])
-            adj_halves[(b, hf)] = half
-
-        sums = {}
-        c_floor = {}
-        root = {}
-        positive = {}
-        d_col = {}
-        d_row = {}
-        half_shape = [P, BLOCKS_PER_HALF]
-
-        def column_sums(b, hf, g):
-            if g == 0:
-                sums[(b, hf)] = psum_aux.tile([P, BLOCKS_PER_HALF, PASSES], F32, name="sums", tag="aux")
-            for blk in range(BLOCKS_PER_HALF):
-                for t in range(PACK):
-                    nc.tensor.matmul(
-                        out=sums[(b, hf)][:, blk, g : g + 1],
-                        lhsT=adj_halves[(b, hf)][:, g * PACK + t, blk * P : (blk + 1) * P],
-                        rhs=ones[:],
-                        start=(t == 0),
-                        stop=(t == PACK - 1),
-                    )
-
-        def degrees_begin(b, hf):
-            c = small.tile(half_shape, F32, name="c", tag="c")
-            nc.vector.tensor_reduce(out=c[:], in_=sums[(b, hf)][:], axis=AXIS.X, op=ALU.add)
-            c_floor[(b, hf)] = small.tile(half_shape, F32, name="c_floor", tag="c_floor")
-            nc.vector.tensor_scalar_max(out=c_floor[(b, hf)][:], in0=c[:], scalar1=1e-30)
-            root[(b, hf)] = small.tile(half_shape, F32, name="root", tag="root")
-            nc.scalar.activation(out=root[(b, hf)][:], in_=c_floor[(b, hf)][:], func=ACT.Sqrt)
-            positive[(b, hf)] = small.tile(half_shape, F32, name="positive", tag="positive")
-            nc.vector.tensor_single_scalar(out=positive[(b, hf)][:], in_=c[:], scalar=0.0, op=ALU.is_gt)
-
-        def degrees_end(b, hf):
-            guess = small.tile(half_shape, F32, name="guess", tag="guess")
-            nc.vector.reciprocal(out=guess[:], in_=root[(b, hf)][:])
-            square = small.tile(half_shape, F32, name="square", tag="square")
-            nc.vector.tensor_mul(out=square[:], in0=guess[:], in1=guess[:])
-            masked = small.tile(half_shape, F32, name="masked", tag="masked")
-            nc.vector.tensor_mul(out=masked[:], in0=guess[:], in1=positive[(b, hf)][:])
-            step = small.tile(half_shape, F32, name="step", tag="step")
-            nc.vector.scalar_tensor_tensor(
-                out=step[:], in0=square[:], scalar=-0.5, in1=c_floor[(b, hf)][:], op0=ALU.mult, op1=ALU.mult
-            )
-            d = degree_pool.tile(half_shape, F32, name="d", tag="d")
-            nc.vector.scalar_tensor_tensor(
-                out=d[:], in0=step[:], scalar=1.5, in1=masked[:], op0=ALU.add, op1=ALU.mult
-            )
-            d_col[(b, hf)] = d
-
-        def spread_rows(b, hf):
-            d_row[(b, hf)] = degree_pool.tile([P, HALF], F32, name="row", tag="row")
-            for q in range(CHUNKS_PER_HALF):
-                spread_ps = psum_aux.tile([P, CHUNK], F32, name="spread_ps", tag="aux")
-                for k in range(BLOCKS_PER_CHUNK):
-                    blk = q * BLOCKS_PER_CHUNK + k
-                    nc.tensor.transpose(
-                        out=spread_ps[:, k * P : (k + 1) * P],
-                        in_=d_col[(b, hf)][:, blk : blk + 1].to_broadcast([P, P]),
-                        identity=ident[:],
-                    )
-                copy = nc.vector.tensor_copy if q % 2 == 0 else nc.scalar.copy
-                copy(out=d_row[(b, hf)][:, q * CHUNK : (q + 1) * CHUNK], in_=spread_ps[:])
+        load_half(0, 1)
+        load_half(1, 0)
+        column_sums(0, 1)
 
         units = []
         for b in range(BATCH):
@@ -190,6 +206,7 @@ def tile_perception_pb_kernel(tc, msg, adj, b2, W3, out):
                 for g in range(PASSES):
                     if chunk >= CHUNKS_PER_HALF or g >= PASSES_PER_HALF:
                         units.append((b, chunk, g))
+        last_chunk = units[-1][0:2]
 
         a_planes = {}
         a_grouped = {}
@@ -218,11 +235,8 @@ def tile_perception_pb_kernel(tc, msg, adj, b2, W3, out):
                 )
             a_planes[(b, chunk, g)] = planes
 
-        def is_last_chunk(b, chunk):
-            return (b, chunk) == (BATCH - 1, CHUNKS - 1)
-
         def regroup_a(b, chunk, g):
-            last_unit = is_last_chunk(b, chunk) and g == PASSES - 1
+            last_unit = (b, chunk) == last_chunk and g == PASSES - 1
             copy = nc.vector.tensor_copy if last_unit else nc.scalar.copy
             a_grouped[(b, chunk, g)] = regroup(copy, a_planes[(b, chunk, g)])
 
@@ -239,12 +253,12 @@ def tile_perception_pb_kernel(tc, msg, adj, b2, W3, out):
         def aggregate(b, chunk, g):
             if chunk < CHUNKS_PER_HALF and g < PASSES_PER_HALF:
                 return
-            first = 0 if (chunk < CHUNKS_PER_HALF and g == PASSES_PER_HALF) else g
-            if first == 0:
+            first_pass = 0 if (chunk < CHUNKS_PER_HALF and g == PASSES_PER_HALF) else g
+            if first_pass == 0:
                 acc[(b, chunk)] = [
                     psum_acc.tile([P, CHUNK], F32, name="acc%d" % ft, tag="acc") for ft in range(F_TILES)
                 ]
-            for gg in range(first, g + 1):
+            for gg in range(first_pass, g + 1):
                 for ft in range(F_TILES):
                     f_cols = slice(ft * P, (ft + 1) * P)
                     nc.tensor.matmul_mx(
@@ -260,7 +274,7 @@ def tile_perception_pb_kernel(tc, msg, adj, b2, W3, out):
         def relu(b, chunk):
             h_planes[(b, chunk)] = work.tile([P, PACK, CHUNK], BF16, name="h_planes", tag="planes")
             for ft in range(F_TILES):
-                if is_last_chunk(b, chunk) and ft % 2 == 1:
+                if (b, chunk) == last_chunk and ft % 2 == 1:
                     nc.vector.tensor_scalar(
                         out=h_planes[(b, chunk)][:, ft, :],
                         in0=acc[(b, chunk)][ft][:],
@@ -303,47 +317,31 @@ def tile_perception_pb_kernel(tc, msg, adj, b2, W3, out):
         def store(b, chunk):
             for it in range(BLOCKS_PER_CHUNK):
                 o_sb = out_pool.tile([P, OUT_DIM], F32, name="o_sb", tag="o_sb")
-                copy = nc.vector.tensor_copy if is_last_chunk(b, chunk) and it % 2 == 1 else nc.scalar.copy
+                copy = nc.vector.tensor_copy if (b, chunk) == last_chunk and it % 2 == 1 else nc.scalar.copy
                 copy(out=o_sb[:], in_=o_ps[(b, chunk, it)][:])
                 first_row = chunk * CHUNK + it * P
                 nc.sync.dma_start(out=out[b, first_row : first_row + P, :], in_=o_sb[:])
-
-        load_half(0, 0)
-        load_half(0, 1)
-        load_half(1, 0)
-        for g in range(PASSES):
-            column_sums(0, 0, g)
-        degrees_begin(0, 0)
-        degrees_end(0, 0)
-        spread_rows(0, 0)
-        for g in range(PASSES):
-            column_sums(0, 1, g)
 
         def prepare(step):
             b, local = divmod(step, UNITS_PER_BATCH)
             if b >= BATCH:
                 return
             if b == 0 and local == EARLY_UNITS:
-                degrees_begin(0, 1)
-                degrees_end(0, 1)
-                spread_rows(0, 1)
+                degrees_begin(b, 1)
+                degrees_end(b, 1)
             if b > 0 and local == 0:
                 degrees_begin(b, 1)
-            if b > 0 and local == 2:
+            if b > 0 and local == DEGREE_GAP:
                 degrees_end(b, 1)
-                spread_rows(b, 1)
             if b + 1 < BATCH:
                 if local == FIRST_HALF_UNITS:
                     load_half(b + 1, 1)
-                if FIRST_HALF_UNITS <= local < FIRST_HALF_UNITS + PASSES:
-                    column_sums(b + 1, 0, local - FIRST_HALF_UNITS)
+                    column_sums(b + 1, 0)
                 if local == FIRST_HALF_UNITS + PASSES:
                     degrees_begin(b + 1, 0)
-                if FIRST_HALF_UNITS + PASSES <= local:
-                    column_sums(b + 1, 1, local - FIRST_HALF_UNITS - PASSES)
-                if local == FIRST_HALF_UNITS + PASSES + 2:
+                    column_sums(b + 1, 1)
+                if local == FIRST_HALF_UNITS + PASSES + DEGREE_GAP:
                     degrees_end(b + 1, 0)
-                    spread_rows(b + 1, 0)
 
         def unit_at(step, lag):
             return units[step - lag] if 0 <= step - lag < len(units) else None
@@ -352,21 +350,21 @@ def tile_perception_pb_kernel(tc, msg, adj, b2, W3, out):
             unit = unit_at(step, lag)
             return unit[0:2] if unit is not None and unit[2] == PASSES - 1 else None
 
-        for step in range(len(units) + 7):
+        for step in range(len(units) + LAG_STORE + 1):
             prepare(step)
             if unit_at(step, 0) is not None:
                 scale(*unit_at(step, 0))
-            if unit_at(step, 1) is not None:
-                regroup_a(*unit_at(step, 1))
-            if closing_at(step, 5) is not None:
-                regroup_h(*closing_at(step, 5))
-            if unit_at(step, 3) is not None:
-                quantise_a(*unit_at(step, 3))
-                aggregate(*unit_at(step, 3))
-            if closing_at(step, 4) is not None:
-                relu(*closing_at(step, 4))
-            if closing_at(step, 5) is not None:
-                quantise_h(*closing_at(step, 5))
-                project(*closing_at(step, 5))
-            if closing_at(step, 6) is not None:
-                store(*closing_at(step, 6))
+            if unit_at(step, LAG_REGROUP) is not None:
+                regroup_a(*unit_at(step, LAG_REGROUP))
+            if closing_at(step, LAG_REQUANTISE) is not None:
+                regroup_h(*closing_at(step, LAG_REQUANTISE))
+            if unit_at(step, LAG_QUANTISE) is not None:
+                quantise_a(*unit_at(step, LAG_QUANTISE))
+                aggregate(*unit_at(step, LAG_QUANTISE))
+            if closing_at(step, LAG_RELU) is not None:
+                relu(*closing_at(step, LAG_RELU))
+            if closing_at(step, LAG_REQUANTISE) is not None:
+                quantise_h(*closing_at(step, LAG_REQUANTISE))
+                project(*closing_at(step, LAG_REQUANTISE))
+            if closing_at(step, LAG_STORE) is not None:
+                store(*closing_at(step, LAG_STORE))

@@ -20,195 +20,213 @@ PACK = 4
 K_PASS = P * PACK
 PASSES = NODES // K_PASS
 ROW_BLOCKS = NODES // P
-HALF = NODES // 2
-HALVES = NODES // HALF
-BLOCKS_PER_HALF = HALF // P
-PASSES_PER_HALF = HALF // K_PASS
 CHUNK = 512
 CHUNKS = NODES // CHUNK
-CHUNKS_PER_HALF = HALF // CHUNK
-BLOCKS_PER_CHUNK = CHUNK // P
+CHUNK_BLOCKS = CHUNK // P
 F_TILES = HIDDEN // P
 RUN = 4
-
-ADJ_BUFS = 3
-LOAD_BLOCKS = 2
-RAW_BUFS = 6
-WORK_BUFS = 5
-
-LAG_REGROUP = 1
-LAG_QUANTISE = LAG_REGROUP + 2
-LAG_RELU = LAG_QUANTISE + 1
-LAG_REQUANTISE = LAG_RELU + 1
-LAG_STORE = LAG_REQUANTISE + 1
-DEGREE_GAP = 2
-
-UNITS_PER_BATCH = CHUNKS * PASSES
-EARLY_UNITS = CHUNKS_PER_HALF * PASSES_PER_HALF
-FIRST_HALF_UNITS = CHUNKS_PER_HALF * PASSES
-
-assert HIDDEN == K_PASS and HIDDEN == CHUNK and OUT_DIM == CHUNK and F_TILES == PACK
+LOAD_BLOCKS = 4
+PARTS = 3
+PAIRS = PARTS * PARTS
+BANK_COLS = 256
+RAW_BUFS = 4
 
 
 def tile_perception_pb_kernel(tc, msg, adj, b2, W3, out):
     nc = tc.nc
     with ExitStack() as ctx:
         keep = ctx.enter_context(tc.tile_pool(name="keep", bufs=1))
-        adj_pool = ctx.enter_context(tc.tile_pool(name="adj_pool", bufs=ADJ_BUFS))
+        adj_pool = ctx.enter_context(tc.tile_pool(name="adj_pool", bufs=5))
         raw_pool = ctx.enter_context(tc.tile_pool(name="raw_pool", bufs=RAW_BUFS))
-        work = ctx.enter_context(tc.tile_pool(name="work", bufs=WORK_BUFS))
+        scaled_pool = ctx.enter_context(tc.tile_pool(name="scaled_pool", bufs=4))
+        planes_pool = ctx.enter_context(tc.tile_pool(name="planes_pool", bufs=2))
+        work = ctx.enter_context(tc.tile_pool(name="work", bufs=4))
+        a_pool = ctx.enter_context(tc.tile_pool(name="a_pool", bufs=3))
         codes_pool = ctx.enter_context(tc.tile_pool(name="codes_pool", bufs=2))
         small = ctx.enter_context(tc.tile_pool(name="small", bufs=2))
-        degree_pool = ctx.enter_context(tc.tile_pool(name="degree_pool", bufs=BATCH * HALVES))
-        out_pool = ctx.enter_context(tc.tile_pool(name="out_pool", bufs=BLOCKS_PER_CHUNK))
-        psum_acc = ctx.enter_context(tc.psum_pool(name="psum_acc", bufs=F_TILES))
-        psum_out = ctx.enter_context(tc.psum_pool(name="psum_out", bufs=2))
-        psum_aux = ctx.enter_context(tc.psum_pool(name="psum_aux", bufs=2))
+        d_pool = ctx.enter_context(tc.tile_pool(name="d_pool", bufs=6))
+        out_pool = ctx.enter_context(tc.tile_pool(name="out_pool", bufs=4))
+        psum_acc = ctx.enter_context(tc.psum_pool(name="psum_acc", bufs=2))
+        psum_factor = ctx.enter_context(tc.psum_pool(name="psum_factor", bufs=3))
+        psum_misc = ctx.enter_context(tc.psum_pool(name="psum_misc", bufs=3))
+        ctx.enter_context(tc.manual_schedule())
 
-        def regroup(copy, planes):
+        def runs(ap, order):
+            return ap.rearrange(order + " -> p c t i", i=RUN)
+
+        def regroup(copy, planes, width):
             grouped = work.tile([P, CHUNK, PACK], BF16, name="grouped", tag="grouped", align_bytes=64)
             copy(
-                out=grouped.rearrange("p (c i) t -> p c t i", i=RUN),
-                in_=planes.rearrange("p t (c i) -> p c t i", i=RUN),
+                out=runs(grouped[:, 0:width, :], "p (c i) t"),
+                in_=runs(planes[:, :, 0:width], "p t (c i)"),
             )
             return grouped
 
-        def quantise(grouped, codes, scales):
+        def quantise(grouped, codes, scales, width):
             nc.vector.quantize_mx(
                 out=codes.bitcast(FP8X4),
                 scales=scales,
-                in_=grouped.rearrange("p w t -> p (w t)"),
+                in_=grouped[:, 0:width, :].rearrange("p w t -> p (w t)"),
             )
 
         warm = keep.tile([P, 1], F32, name="warm")
         nc.vector.memset(warm[:], 1.0)
-        nc.scalar.activation(out=warm[:], in_=warm[:], func=ACT.Sqrt)
-        ident = keep.tile([P, P], F32, name="ident")
-        make_identity(nc, ident[:])
+        nc.scalar.activation(out=warm[:], in_=warm[:], func=ACT.Abs_reciprocal_sqrt)
         ones = keep.tile([P, 1], BF16, name="ones")
         nc.vector.memset(ones[:], 1.0)
+        ident = keep.tile([P, P], F32, name="ident")
+        make_identity(nc, ident[:])
+        ident_bf = keep.tile([P, P], BF16, name="ident_bf")
+        make_identity(nc, ident_bf[:])
+        b2_rows = keep.tile([P, P], BF16, name="b2_rows")
+        nc.gpsimd.memset(b2_rows[:], 0.0)
+        left_cols = keep.tile([P, CHUNK_BLOCKS, P], BF16, name="left_cols")
+        nc.gpsimd.memset(left_cols[:], 0.0)
+        right_cols = keep.tile([P, CHUNK_BLOCKS, P], BF16, name="right_cols")
+        nc.gpsimd.memset(right_cols[:], 0.0)
+        b2_col = keep.tile([P, PACK], F32, name="b2_col")
 
-        adj_halves = {}
+        def load_b2():
+            nc.sync.dma_start(out=b2_rows[0:PACK, :], in_=b2.rearrange("(t p) -> t p", p=P))
+
+        def turn_b2():
+            b2_ps = psum_misc.tile([P, P], BF16, name="b2_ps", tag="misc")
+            nc.tensor.transpose(out=b2_ps[:], in_=b2_rows[:], identity=ident_bf[:])
+            nc.scalar.copy(out=b2_col[:], in_=b2_ps[:, 0:PACK])
+
+        adj_chunks = {}
         sums = {}
-        c_floor = {}
-        root = {}
-        positive = {}
         d_col = {}
         d_row = {}
-        half_shape = [P, BLOCKS_PER_HALF]
+        left_rows = {}
+        right_rows = {}
 
-        def load_half(b, hf):
-            half = adj_pool.tile([P, ROW_BLOCKS, HALF], BF16, name="half", tag="half")
+        def load_chunk(b, q):
+            chunk = adj_pool.tile([P, ROW_BLOCKS, CHUNK], BF16, name="chunk", tag="chunk")
             rows = adj[b].rearrange("(k p) i -> p k i", p=P)
             for first in range(0, ROW_BLOCKS, LOAD_BLOCKS):
                 blocks = slice(first, first + LOAD_BLOCKS)
-                nc.sync.dma_start(out=half[:, blocks, :], in_=rows[:, blocks, hf * HALF : (hf + 1) * HALF])
-            adj_halves[(b, hf)] = half
+                nc.sync.dma_start(out=chunk[:, blocks, :], in_=rows[:, blocks, q * CHUNK : (q + 1) * CHUNK])
+            adj_chunks[(b, q)] = chunk
 
-        def column_sums(b, hf):
-            sums[(b, hf)] = psum_aux.tile([P, BLOCKS_PER_HALF, ROW_BLOCKS], F32, name="sums", tag="aux")
-            for k in range(ROW_BLOCKS):
-                for blk in range(BLOCKS_PER_HALF):
+        def column_sums(b, q, ks):
+            if ks[0] == 0:
+                sums[(b, q)] = psum_misc.tile([P, CHUNK_BLOCKS, ROW_BLOCKS], F32, name="sums", tag="misc")
+            for k in ks:
+                for n in range(CHUNK_BLOCKS):
                     nc.tensor.matmul(
-                        out=sums[(b, hf)][:, blk, k : k + 1],
-                        lhsT=adj_halves[(b, hf)][:, k, blk * P : (blk + 1) * P],
+                        out=sums[(b, q)][:, n, k : k + 1],
+                        lhsT=adj_chunks[(b, q)][:, k, n * P : (n + 1) * P],
                         rhs=ones[:],
                         start=True,
                         stop=True,
                     )
 
-        def degrees_begin(b, hf):
-            c = small.tile(half_shape, F32, name="c", tag="c")
-            nc.vector.tensor_reduce(out=c[:], in_=sums[(b, hf)][:], axis=AXIS.X, op=ALU.add)
-            c_floor[(b, hf)] = small.tile(half_shape, F32, name="c_floor", tag="c_floor")
-            nc.vector.tensor_scalar_max(out=c_floor[(b, hf)][:], in0=c[:], scalar1=1e-30)
-            root[(b, hf)] = small.tile(half_shape, F32, name="root", tag="root")
-            nc.scalar.activation(out=root[(b, hf)][:], in_=c_floor[(b, hf)][:], func=ACT.Sqrt)
-            positive[(b, hf)] = small.tile(half_shape, F32, name="positive", tag="positive")
-            nc.vector.tensor_single_scalar(out=positive[(b, hf)][:], in_=c[:], scalar=0.0, op=ALU.is_gt)
+        shape = [P, CHUNK_BLOCKS]
 
-        def degrees_end(b, hf):
-            guess = small.tile(half_shape, F32, name="guess", tag="guess")
-            nc.vector.reciprocal(out=guess[:], in_=root[(b, hf)][:])
-            square = small.tile(half_shape, F32, name="square", tag="square")
-            nc.vector.tensor_mul(out=square[:], in0=guess[:], in1=guess[:])
-            masked = small.tile(half_shape, F32, name="masked", tag="masked")
-            nc.vector.tensor_mul(out=masked[:], in0=guess[:], in1=positive[(b, hf)][:])
-            step = small.tile(half_shape, F32, name="step", tag="step")
-            nc.vector.scalar_tensor_tensor(
-                out=step[:], in0=square[:], scalar=-0.5, in1=c_floor[(b, hf)][:], op0=ALU.mult, op1=ALU.mult
+        def degrees(b, q, engine):
+            c = small.tile(shape, F32, name="c", tag="c")
+            nc.vector.tensor_reduce(out=c[:], in_=sums[(b, q)][:], axis=AXIS.X, op=ALU.add)
+            c_floor = small.tile(shape, F32, name="c_floor", tag="c_floor")
+            engine.tensor_scalar_max(out=c_floor[:], in0=c[:], scalar1=1e-30)
+            guess = small.tile(shape, F32, name="guess", tag="guess")
+            nc.scalar.activation(out=guess[:], in_=c_floor[:], func=ACT.Abs_reciprocal_sqrt)
+            positive = small.tile(shape, F32, name="positive", tag="positive")
+            engine.tensor_single_scalar(out=positive[:], in_=c[:], scalar=0.0, op=ALU.is_gt)
+            square = small.tile(shape, F32, name="square", tag="square")
+            engine.tensor_mul(out=square[:], in0=guess[:], in1=guess[:])
+            product = small.tile(shape, F32, name="product", tag="product")
+            engine.tensor_mul(out=product[:], in0=square[:], in1=c_floor[:])
+            masked = small.tile(shape, F32, name="masked", tag="masked")
+            engine.tensor_mul(out=masked[:], in0=guess[:], in1=positive[:])
+            newton = small.tile(shape, F32, name="newton", tag="newton")
+            engine.tensor_scalar(
+                out=newton[:], in0=product[:], scalar1=-0.5, scalar2=1.5, op0=ALU.mult, op1=ALU.add
             )
-            d_col[(b, hf)] = degree_pool.tile(half_shape, F32, name="d", tag="d")
-            nc.vector.scalar_tensor_tensor(
-                out=d_col[(b, hf)][:], in0=step[:], scalar=1.5, in1=masked[:], op0=ALU.add, op1=ALU.mult
-            )
-            d_row[(b, hf)] = degree_pool.tile([P, HALF], F32, name="row", tag="row")
-            for q in range(CHUNKS_PER_HALF):
-                spread_ps = psum_aux.tile([P, CHUNK], F32, name="spread_ps", tag="aux")
-                for n in range(BLOCKS_PER_CHUNK):
-                    blk = q * BLOCKS_PER_CHUNK + n
-                    nc.tensor.transpose(
-                        out=spread_ps[:, n * P : (n + 1) * P],
-                        in_=d_col[(b, hf)][:, blk : blk + 1].to_broadcast([P, P]),
-                        identity=ident[:],
-                    )
-                nc.scalar.copy(out=d_row[(b, hf)][:, q * CHUNK : (q + 1) * CHUNK], in_=spread_ps[:])
+            d_col[(b, q)] = d_pool.tile(shape, F32, name="d", tag="d")
+            engine.tensor_mul(out=d_col[(b, q)][:], in0=newton[:], in1=masked[:])
 
-        load_half(0, 0)
-        column_sums(0, 0)
-        degrees_begin(0, 0)
-        degrees_end(0, 0)
+        def spread(b, q):
+            spread_ps = psum_misc.tile([P, CHUNK], F32, name="spread_ps", tag="misc")
+            for n in range(CHUNK_BLOCKS):
+                nc.tensor.transpose(
+                    out=spread_ps[:, n * P : (n + 1) * P],
+                    in_=d_col[(b, q)][:, n : n + 1].to_broadcast([P, P]),
+                    identity=ident[:],
+                )
+            d_row[(b, q)] = d_pool.tile([P, CHUNK], F32, name="row", tag="row")
+            nc.scalar.copy(out=d_row[(b, q)][:], in_=spread_ps[:])
 
-        b2_rows = keep.tile([P, P], BF16, name="b2_rows")
-        nc.vector.memset(b2_rows[:], 0.0)
-        nc.sync.dma_start(out=b2_rows[0:PACK, :], in_=b2.rearrange("(t p) -> t p", p=P))
-        b2_rows_f32 = keep.tile([P, P], F32, name="b2_rows_f32")
-        nc.vector.tensor_copy(out=b2_rows_f32[:], in_=b2_rows[:])
-        b2_ps = psum_aux.tile([P, P], F32, name="b2_ps", tag="aux")
-        nc.tensor.transpose(out=b2_ps[:], in_=b2_rows_f32[:], identity=ident[:])
-        b2_col = keep.tile([P, PACK], F32, name="b2_col")
-        nc.vector.tensor_copy(out=b2_col[:], in_=b2_ps[:, 0:PACK])
+        def split(b, q):
+            d = d_col[(b, q)]
+            parts = small.tile([P, CHUNK_BLOCKS, PARTS], BF16, name="parts", tag="parts")
+            rest = small.tile(shape, F32, name="rest", tag="rest")
+            nc.gpsimd.tensor_copy(out=parts[:, :, 0], in_=d[:])
+            nc.gpsimd.tensor_tensor(out=rest[:], in0=d[:], in1=parts[:, :, 0], op=ALU.subtract)
+            nc.gpsimd.tensor_copy(out=parts[:, :, 1], in_=rest[:])
+            nc.gpsimd.tensor_tensor(out=parts[:, :, 2], in0=rest[:], in1=parts[:, :, 1], op=ALU.subtract)
+            for cols, axis in ((left_cols, 2), (right_cols, 3)):
+                nc.gpsimd.tensor_copy(
+                    out=cols[:, :, 0:PAIRS].rearrange("p k (a c) -> p k a c", a=PARTS),
+                    in_=parts[:].unsqueeze(axis).to_broadcast([P, CHUNK_BLOCKS, PARTS, PARTS]),
+                )
+
+        def turn_parts(b, q, cols, rows, tag):
+            rows_ps = psum_misc.tile([P, CHUNK], BF16, name="rows_ps", tag="misc")
+            for n in range(CHUNK_BLOCKS):
+                nc.tensor.transpose(
+                    out=rows_ps[:, n * P : (n + 1) * P], in_=cols[:, n, :], identity=ident_bf[:]
+                )
+            rows[(b, q)] = d_pool.tile([P, CHUNK], BF16, name=tag, tag=tag)
+            nc.scalar.copy(out=rows[(b, q)][:], in_=rows_ps[:])
+
+        def turn_left(b, q):
+            turn_parts(b, q, left_cols, left_rows, "left")
+
+        def turn_right(b, q):
+            turn_parts(b, q, right_cols, right_rows, "right")
 
         msg_codes = keep.tile([P, BATCH, PASSES, HIDDEN], U32, name="msg_codes", align_bytes=64)
         msg_scales = keep.tile([P, BATCH, PASSES, HIDDEN], U8, name="msg_scales", align_bytes=64)
         w3_codes = keep.tile([P, OUT_DIM], U32, name="w3_codes", align_bytes=64)
         w3_scales = keep.tile([P, OUT_DIM], U8, name="w3_scales", align_bytes=64)
-        pieces = []
+        w3_piece = (W3.rearrange("(t p) d -> p t d", p=P), w3_codes[:], w3_scales[:])
+        msg_pieces = []
         for b in range(BATCH):
             rows = msg[b].rearrange("(g t p) f -> g p t f", t=PACK, p=P)
-            for g in range(PASSES):
-                pieces.append((rows[g], msg_codes[:, b, g, :], msg_scales[:, b, g, :]))
-        pieces.append((W3.rearrange("(t p) d -> p t d", p=P), w3_codes[:], w3_scales[:]))
+            msg_pieces.append([(rows[g], msg_codes[:, b, g, :], msg_scales[:, b, g, :]) for g in range(PASSES)])
+        pieces = msg_pieces[0] + [w3_piece] + msg_pieces[1]
         raws = {}
         piece_grouped = {}
-        for n in range(len(pieces) + RAW_BUFS + 1):
-            if 0 <= n - RAW_BUFS - 1:
-                source, codes, scales = pieces[n - RAW_BUFS - 1]
-                quantise(piece_grouped[n - RAW_BUFS - 1], codes, scales)
-            if 0 <= n - RAW_BUFS < len(pieces):
-                copy = nc.vector.tensor_copy if n % 2 == 0 else nc.scalar.copy
-                piece_grouped[n - RAW_BUFS] = regroup(copy, raws[n - RAW_BUFS])
-            if n < len(pieces):
-                source, codes, scales = pieces[n]
-                raws[n] = raw_pool.tile([P, PACK, CHUNK], BF16, name="raw", tag="raw")
-                nc.sync.dma_start(out=raws[n][:], in_=source)
 
-        load_half(0, 1)
-        load_half(1, 0)
-        column_sums(0, 1)
+        def load_piece(n):
+            raws[n] = raw_pool.tile([P, PACK, CHUNK], BF16, name="raw", tag="raw")
+            nc.sync.dma_start(out=raws[n][:], in_=pieces[n][0])
 
+        def regroup_piece(n, copy):
+            piece_grouped[n] = regroup(copy, raws[n], CHUNK)
+
+        def quantise_piece(n):
+            quantise(piece_grouped[n], pieces[n][1], pieces[n][2], CHUNK)
+
+        chunks = []
         units = []
         for b in range(BATCH):
-            for chunk in range(CHUNKS_PER_HALF):
-                for g in range(PASSES_PER_HALF):
-                    units.append((b, chunk, g))
-            for chunk in range(CHUNKS):
-                for g in range(PASSES):
-                    if chunk >= CHUNKS_PER_HALF or g >= PASSES_PER_HALF:
-                        units.append((b, chunk, g))
-        last_chunk = units[-1][0:2]
+            first = len(chunks)
+            widths = [CHUNK] * 4 if b + 1 < BATCH else [CHUNK] * 3 + [CHUNK // 2] * 2
+            col = 0
+            for width in widths:
+                chunks.append((b, col, width))
+                col += width
+            for gs in ((0, 1), (2,), (3,)):
+                for n in (first, first + 1):
+                    units += [(n, g) for g in gs]
+            for n in range(first + 2, len(chunks)):
+                units += [(n, g) for g in range(PASSES)]
+        last_chunk = len(chunks) - 1
 
-        a_planes = {}
+        made = {}
+        factors = {}
         a_grouped = {}
         a_codes = {}
         a_scales = {}
@@ -217,67 +235,105 @@ def tile_perception_pb_kernel(tc, msg, adj, b2, W3, out):
         h_grouped = {}
         h_codes = {}
         h_scales = {}
-        o_ps = {}
+        o_banks = {}
 
-        def scale(b, chunk, g):
-            hf_cols, first_col = divmod(chunk * CHUNK, HALF)
-            cols = slice(first_col, first_col + CHUNK)
-            planes = work.tile([P, PACK, CHUNK], BF16, name="planes", tag="planes")
-            for t in range(PACK):
-                hf_rows, blk = divmod(g * PACK + t, BLOCKS_PER_HALF)
-                nc.vector.scalar_tensor_tensor(
-                    out=planes[:, t, :],
-                    in0=adj_halves[(b, hf_cols)][:, g * PACK + t, cols],
-                    scalar=d_col[(b, hf_rows)][:, blk : blk + 1],
-                    in1=d_row[(b, hf_cols)][:, cols],
-                    op0=ALU.mult,
-                    op1=ALU.mult,
+        def kind(n, g):
+            c = chunks[n][1] // CHUNK
+            if (n, g) == units[0]:
+                return "scalar"
+            if (c + g) % 2 == 0:
+                return "matmul"
+            return "scalar" if c < g else "mirror"
+
+        def factor_by_scalar(n, g, ts):
+            b, c = chunks[n][0], chunks[n][1] // CHUNK
+            if ts[0] == 0:
+                made[(b, c, g)] = scaled_pool.tile([P, PACK, CHUNK], BF16, name="scaled", tag="scaled")
+            planes = made[(b, c, g)]
+            for t in ts:
+                nc.scalar.activation(
+                    out=planes[:, t, :], in_=d_row[(b, c)][:], func=ACT.Copy, scale=d_col[(b, g)][:, t : t + 1]
                 )
-            a_planes[(b, chunk, g)] = planes
+            for m, (batch, start, width) in enumerate(chunks):
+                if batch == b and start // CHUNK == c:
+                    first = start % CHUNK
+                    factors[(m, g)] = [planes[:, :, col : col + BANK_COLS] for col in range(first, first + width, BANK_COLS)]
 
-        def regroup_a(b, chunk, g):
-            last_unit = (b, chunk) == last_chunk and g == PASSES - 1
-            copy = nc.vector.tensor_copy if last_unit else nc.scalar.copy
-            a_grouped[(b, chunk, g)] = regroup(copy, a_planes[(b, chunk, g)])
-
-        def quantise_a(b, chunk, g):
-            if g == 0:
-                a_codes[(b, chunk)] = codes_pool.tile(
-                    [P, PASSES, CHUNK], U32, name="a_codes", tag="a_codes", align_bytes=64
-                )
-                a_scales[(b, chunk)] = codes_pool.tile(
-                    [P, PASSES, CHUNK], U8, name="a_scales", tag="a_scales", align_bytes=64
-                )
-            quantise(a_grouped[(b, chunk, g)], a_codes[(b, chunk)][:, g, :], a_scales[(b, chunk)][:, g, :])
-
-        def aggregate(b, chunk, g):
-            if chunk < CHUNKS_PER_HALF and g < PASSES_PER_HALF:
+        def factor_by_tensor(n, g, k):
+            b, first_col, width = chunks[n]
+            if k * BANK_COLS >= width:
                 return
-            first_pass = 0 if (chunk < CHUNKS_PER_HALF and g == PASSES_PER_HALF) else g
-            if first_pass == 0:
-                acc[(b, chunk)] = [
-                    psum_acc.tile([P, CHUNK], F32, name="acc%d" % ft, tag="acc") for ft in range(F_TILES)
-                ]
-            for gg in range(first_pass, g + 1):
-                for ft in range(F_TILES):
+            c, col = divmod(first_col + k * BANK_COLS, CHUNK)
+            bank = psum_factor.tile([P, PACK, BANK_COLS], BF16, name="bank", tag="bank")
+            for t in range(PACK):
+                if kind(n, g) == "matmul":
+                    nc.tensor.matmul(
+                        out=bank[:, t, :],
+                        lhsT=left_rows[(b, g)][:, t * P : (t + 1) * P],
+                        rhs=right_rows[(b, c)][:, col : col + BANK_COLS],
+                        start=True,
+                        stop=True,
+                    )
+                    continue
+                for m in range(BANK_COLS // P):
+                    nc.tensor.transpose(
+                        out=bank[:, t, m * P : (m + 1) * P],
+                        in_=made[(b, g, c)][:, col // P + m, t * P : (t + 1) * P],
+                        identity=ident_bf[:],
+                    )
+            factors.setdefault((n, g), []).append(bank)
+
+        def scale(n, g):
+            b, first_col, width = chunks[n]
+            c, local = divmod(first_col, CHUNK)
+            grouped = work.tile([P, CHUNK, PACK], BF16, name="grouped", tag="grouped", align_bytes=64)
+            rows = slice(g * PACK, (g + 1) * PACK)
+            for k in range(width // BANK_COLS):
+                cols = slice(local + k * BANK_COLS, local + (k + 1) * BANK_COLS)
+                nc.vector.tensor_tensor(
+                    out=runs(grouped[:, k * BANK_COLS : (k + 1) * BANK_COLS, :], "p (c i) t"),
+                    in0=runs(adj_chunks[(b, c)][:, rows, cols], "p t (c i)"),
+                    in1=runs(factors[(n, g)][k], "p t (c i)"),
+                    op=ALU.mult,
+                )
+            a_grouped[(n, g)] = grouped
+
+        def quantise_a(n, g):
+            width = chunks[n][2]
+            if n not in a_codes:
+                a_codes[n] = a_pool.tile([P, PASSES, CHUNK], U32, name="a_codes", tag="a_codes", align_bytes=64)
+                a_scales[n] = a_pool.tile([P, PASSES, CHUNK], U8, name="a_scales", tag="a_scales", align_bytes=64)
+            quantise(a_grouped[(n, g)], a_codes[n][:, g, 0:width], a_scales[n][:, g, 0:width], width)
+
+        def aggregate(n, pair, passes):
+            b, first_col, width = chunks[n]
+            for ft in pair:
+                if passes[0] == 0 and n == last_chunk and ft >= 2:
+                    acc[(n, ft)] = psum_factor.tile([P, CHUNK], F32, name="acc", tag="bank")
+                elif passes[0] == 0:
+                    acc[(n, ft)] = psum_acc.tile([P, CHUNK], F32, name="acc", tag="acc")
+            for g in passes:
+                for ft in pair:
                     f_cols = slice(ft * P, (ft + 1) * P)
                     nc.tensor.matmul_mx(
-                        out=acc[(b, chunk)][ft][:],
-                        lhsT=msg_codes[:, b, gg, f_cols].bitcast(FP8X4),
-                        lhsT_scale=msg_scales[:, b, gg, f_cols],
-                        rhs=a_codes[(b, chunk)][:, gg, :].bitcast(FP8X4),
-                        rhs_scale=a_scales[(b, chunk)][:, gg, :],
-                        start=(gg == 0),
-                        stop=(gg == PASSES - 1),
+                        out=acc[(n, ft)][:, 0:width],
+                        lhsT=msg_codes[:, b, g, f_cols].bitcast(FP8X4),
+                        lhsT_scale=msg_scales[:, b, g, f_cols],
+                        rhs=a_codes[n][:, g, 0:width].bitcast(FP8X4),
+                        rhs_scale=a_scales[n][:, g, 0:width],
+                        start=(g == 0),
+                        stop=(g == PASSES - 1),
                     )
 
-        def relu(b, chunk):
-            h_planes[(b, chunk)] = work.tile([P, PACK, CHUNK], BF16, name="h_planes", tag="planes")
-            for ft in range(F_TILES):
-                if (b, chunk) == last_chunk and ft % 2 == 1:
+        def relu(n, pair):
+            width = chunks[n][2]
+            if pair[0] == 0:
+                h_planes[n] = planes_pool.tile([P, PACK, CHUNK], BF16, name="h_planes", tag="planes")
+            for ft in pair:
+                if n == last_chunk and ft % 2 == 1:
                     nc.vector.tensor_scalar(
-                        out=h_planes[(b, chunk)][:, ft, :],
-                        in0=acc[(b, chunk)][ft][:],
+                        out=h_planes[n][:, ft, 0:width],
+                        in0=acc[(n, ft)][:, 0:width],
                         scalar1=b2_col[:, ft : ft + 1],
                         scalar2=0.0,
                         op0=ALU.add,
@@ -285,86 +341,188 @@ def tile_perception_pb_kernel(tc, msg, adj, b2, W3, out):
                     )
                 else:
                     nc.scalar.activation(
-                        out=h_planes[(b, chunk)][:, ft, :],
-                        in_=acc[(b, chunk)][ft][:],
+                        out=h_planes[n][:, ft, 0:width],
+                        in_=acc[(n, ft)][:, 0:width],
                         func=ACT.Relu,
                         bias=b2_col[:, ft : ft + 1],
                         scale=1.0,
                     )
 
-        def regroup_h(b, chunk):
-            h_grouped[(b, chunk)] = regroup(nc.vector.tensor_copy, h_planes[(b, chunk)])
-
-        def quantise_h(b, chunk):
-            h_codes[(b, chunk)] = codes_pool.tile([P, CHUNK], U32, name="h_codes", tag="h_codes", align_bytes=64)
-            h_scales[(b, chunk)] = codes_pool.tile([P, CHUNK], U8, name="h_scales", tag="h_scales", align_bytes=64)
-            quantise(h_grouped[(b, chunk)], h_codes[(b, chunk)][:], h_scales[(b, chunk)][:])
-
-        def project(b, chunk):
-            for it in range(BLOCKS_PER_CHUNK):
-                i_cols = slice(it * P, (it + 1) * P)
-                o_ps[(b, chunk, it)] = psum_out.tile([P, OUT_DIM], F32, name="o_ps", tag="o_ps")
-                nc.tensor.matmul_mx(
-                    out=o_ps[(b, chunk, it)][:],
-                    lhsT=h_codes[(b, chunk)][:, i_cols].bitcast(FP8X4),
-                    lhsT_scale=h_scales[(b, chunk)][:, i_cols],
-                    rhs=w3_codes[:].bitcast(FP8X4),
-                    rhs_scale=w3_scales[:],
-                    start=True,
-                    stop=True,
+        def regroup_h(n, half):
+            copy = nc.vector.tensor_copy if n >= last_chunk - TAIL else nc.scalar.copy
+            cols = slice(half * chunks[n][2] // 2, (half + 1) * chunks[n][2] // 2)
+            if half == 0:
+                h_grouped[n] = planes_pool.tile(
+                    [P, CHUNK, PACK], BF16, name="h_grouped", tag="h_grouped", align_bytes=64
                 )
+            copy(out=runs(h_grouped[n][:, cols, :], "p (c i) t"), in_=runs(h_planes[n][:, :, cols], "p t (c i)"))
 
-        def store(b, chunk):
-            for it in range(BLOCKS_PER_CHUNK):
-                o_sb = out_pool.tile([P, OUT_DIM], F32, name="o_sb", tag="o_sb")
-                copy = nc.vector.tensor_copy if (b, chunk) == last_chunk and it % 2 == 1 else nc.scalar.copy
-                copy(out=o_sb[:], in_=o_ps[(b, chunk, it)][:])
-                first_row = chunk * CHUNK + it * P
-                nc.sync.dma_start(out=out[b, first_row : first_row + P, :], in_=o_sb[:])
+        def quantise_h(n):
+            width = chunks[n][2]
+            h_codes[n] = codes_pool.tile([P, CHUNK], U32, name="h_codes", tag="h_codes", align_bytes=64)
+            h_scales[n] = codes_pool.tile([P, CHUNK], U8, name="h_scales", tag="h_scales", align_bytes=64)
+            quantise(h_grouped[n], h_codes[n][:, 0:width], h_scales[n][:, 0:width], width)
 
-        def prepare(step):
-            b, local = divmod(step, UNITS_PER_BATCH)
-            if b >= BATCH:
-                return
-            if b == 0 and local == EARLY_UNITS:
-                degrees_begin(b, 1)
-                degrees_end(b, 1)
-            if b > 0 and local == 0:
-                degrees_begin(b, 1)
-            if b > 0 and local == DEGREE_GAP:
-                degrees_end(b, 1)
-            if b + 1 < BATCH:
-                if local == FIRST_HALF_UNITS:
-                    load_half(b + 1, 1)
-                    column_sums(b + 1, 0)
-                if local == FIRST_HALF_UNITS + PASSES:
-                    degrees_begin(b + 1, 0)
-                    column_sums(b + 1, 1)
-                if local == FIRST_HALF_UNITS + PASSES + DEGREE_GAP:
-                    degrees_end(b + 1, 0)
+        def project(n, it):
+            b, first_col, width = chunks[n]
+            i_cols = slice(it * P, (it + 1) * P)
+            o_ps = psum_misc.tile([P, OUT_DIM], F32, name="o_ps", tag="misc")
+            nc.tensor.matmul_mx(
+                out=o_ps[:],
+                lhsT=h_codes[n][:, i_cols].bitcast(FP8X4),
+                lhsT_scale=h_scales[n][:, i_cols],
+                rhs=w3_codes[:].bitcast(FP8X4),
+                rhs_scale=w3_scales[:],
+                start=True,
+                stop=True,
+            )
+            o_banks[(n, it)] = o_ps
 
-        def unit_at(step, lag):
-            return units[step - lag] if 0 <= step - lag < len(units) else None
+        def store(n, it):
+            b, first_col, width = chunks[n]
+            o_sb = out_pool.tile([P, OUT_DIM], F32, name="o_sb", tag="o_sb")
+            copy = nc.vector.tensor_copy if n == last_chunk and it % 2 == 1 else nc.scalar.copy
+            copy(out=o_sb[:], in_=o_banks[(n, it)][:])
+            first_row = first_col + it * P
+            nc.sync.dma_start(out=out[b, first_row : first_row + P, :], in_=o_sb[:])
 
-        def closing_at(step, lag):
-            unit = unit_at(step, lag)
-            return unit[0:2] if unit is not None and unit[2] == PASSES - 1 else None
+        load_chunk(0, 0)
+        load_chunk(0, 1)
+        load_piece(0)
+        load_piece(1)
+        load_piece(2)
+        load_chunk(0, 2)
+        load_piece(3)
+        load_chunk(0, 3)
+        load_b2()
+        load_chunk(1, 0)
 
-        for step in range(len(units) + LAG_STORE + 1):
-            prepare(step)
-            if unit_at(step, 0) is not None:
-                scale(*unit_at(step, 0))
-            if unit_at(step, LAG_REGROUP) is not None:
-                regroup_a(*unit_at(step, LAG_REGROUP))
-            if closing_at(step, LAG_REQUANTISE) is not None:
-                regroup_h(*closing_at(step, LAG_REQUANTISE))
-            if unit_at(step, LAG_QUANTISE) is not None:
-                quantise_a(*unit_at(step, LAG_QUANTISE))
-                aggregate(*unit_at(step, LAG_QUANTISE))
-            if closing_at(step, LAG_RELU) is not None:
-                relu(*closing_at(step, LAG_RELU))
-            if closing_at(step, LAG_REQUANTISE) is not None:
-                quantise_h(*closing_at(step, LAG_REQUANTISE))
-                project(*closing_at(step, LAG_REQUANTISE))
-            if closing_at(step, LAG_STORE) is not None:
-                store(*closing_at(step, LAG_STORE))
+        column_sums(0, 0, range(ROW_BLOCKS))
+        degrees(0, 0, nc.vector)
+        spread(0, 0)
+        split(0, 0)
+        factor_by_scalar(*units[0], range(PACK))
+        column_sums(0, 1, range(ROW_BLOCKS))
+        degrees(0, 1, nc.vector)
+        spread(0, 1)
+        factor_by_scalar(*units[1], range(PACK))
+        turn_left(0, 0)
+        turn_right(0, 0)
+        split(0, 1)
+        turn_left(0, 1)
+        turn_right(0, 1)
+
+        degree_steps = {
+            (0, 2): (1, 2, 3, 3),
+            (0, 3): (2, 3, 4, 5),
+            (1, 0): (8, 10, 11, 13),
+            (1, 1): (11, 13, 14, 16),
+            (1, 2): (13, 16, 17, 19),
+            (1, 3): (16, 19, 20, 22),
+        }
+        regroups = {0: 0, 2: 1, 1: 1, 3: 2, 4: 4, 5: 6, 6: 8, 7: 10, 8: 12}
+        AHEAD = 5
+        waiting = []
+        for index in range(2, len(units)):
+            n, g = units[index]
+            if kind(n, g) == "scalar" and chunks[n][1] % CHUNK == 0:
+                waiting += [(index, *units[index], range(0, 2)), (index, *units[index], range(2, 4))]
+        TAIL = 1
+        starts = {}
+        pairs = ((0, 1), (2, 3))
+        banks = []
+        for index, (n, g) in enumerate(units):
+            if kind(n, g) != "scalar":
+                banks += [(index, n, g, k) for k in range(chunks[n][2] // BANK_COLS)]
+
+        def make_banks(step, limit):
+            pending = len([1 for n, g in factors for bank in factors[(n, g)] if units.index((n, g)) > step and kind(n, g) != "scalar"])
+            while banks and pending < limit:
+                index, n, g, k = banks[0]
+                b, c = chunks[n][0], chunks[n][1] // CHUNK
+                if kind(n, g) == "mirror":
+                    if (b, g, c) not in made:
+                        return
+                elif (b, g) not in left_rows or (b, c) not in right_rows:
+                    return
+                factor_by_tensor(n, g, k)
+                banks.remove(banks[0])
+                pending += 1
+
+        for step in range(len(units) + 14):
+            for q, at in ((1, 7), (2, 8), (3, 12)):
+                if step == at:
+                    load_chunk(1, q)
+            for key, at in degree_steps.items():
+                if step == at[1]:
+                    degrees(*key, nc.gpsimd)
+            for n, at in regroups.items():
+                if step == at and n % 2 == 0:
+                    regroup_piece(n, nc.vector.tensor_copy)
+            if step < len(units):
+                scale(*units[step])
+            for n, at in regroups.items():
+                if step == at + 1 + n % 2:
+                    quantise_piece(n)
+                    if n + RAW_BUFS < len(pieces):
+                        load_piece(n + RAW_BUFS)
+            if 0 <= step - 1 < len(units):
+                n, g = units[step - 1]
+                quantise_a(n, g)
+                if g == PASSES - 1:
+                    starts[n] = max(step + 1, starts[n - 1] + 3) if n > 0 else step + 1
+            for n, at in starts.items():
+                if step == at + 5:
+                    quantise_h(n)
+            for n, at in starts.items():
+                if 0 <= step - at - 7 < chunks[n][2] // P:
+                    store(n, step - at - 7)
+            for n, at in starts.items():
+                if step == at + 1:
+                    relu(n, pairs[0])
+                if step == at + 2:
+                    relu(n, pairs[1])
+                for half in range(2):
+                    if step == at + 3 + half:
+                        regroup_h(n, half)
+            for key, at in degree_steps.items():
+                if step == at[2]:
+                    spread(*key)
+                if step == at[3]:
+                    turn_left(*key)
+            make_banks(step, 1)
+            for n, at in starts.items():
+                if 0 <= step - at - 6 < chunks[n][2] // P:
+                    project(n, step - at - 6)
+            for key, at in degree_steps.items():
+                if step == at[3]:
+                    turn_right(*key)
+            make_banks(step, 2)
+            for n, at in starts.items():
+                if n < last_chunk and step == at:
+                    aggregate(n, pairs[0], range(PASSES))
+                if n < last_chunk and step == at + 1:
+                    aggregate(n, pairs[1], range(PASSES))
+            if step >= len(units) - PASSES + 2 and step < len(units) + 2:
+                g = step - (len(units) - PASSES + 2)
+                for pair in pairs:
+                    aggregate(last_chunk, pair, range(g, g + 1))
+            make_banks(step, 3)
+            for key, at in degree_steps.items():
+                if step == at[0]:
+                    column_sums(*key, range(ROW_BLOCKS))
+            for key, at in degree_steps.items():
+                if step == at[1]:
+                    split(*key)
+            for n, at in regroups.items():
+                if step == at and n % 2 == 1:
+                    regroup_piece(n, nc.scalar.copy)
+            emitted = 0
+            for index, n, g, ts in waiting[:]:
+                b, c = chunks[n][0], chunks[n][1] // CHUNK
+                if (b, g) in d_col and (b, c) in d_row and (index <= step + 1 or (emitted == 0 and index <= step + AHEAD)):
+                    factor_by_scalar(n, g, ts)
+                    waiting.remove((index, n, g, ts))
+                    emitted += 1
+            if step == 4:
+                turn_b2()

@@ -38,7 +38,7 @@ def tile_perception_pb_kernel(tc, msg, adj, b2, W3, out):
         keep = ctx.enter_context(tc.tile_pool(name="keep", bufs=1))
         adj_pool = ctx.enter_context(tc.tile_pool(name="adj_pool", bufs=5))
         raw_pool = ctx.enter_context(tc.tile_pool(name="raw_pool", bufs=RAW_BUFS))
-        scaled_pool = ctx.enter_context(tc.tile_pool(name="scaled_pool", bufs=4))
+        scaled_pool = ctx.enter_context(tc.tile_pool(name="scaled_pool", bufs=5))
         planes_pool = ctx.enter_context(tc.tile_pool(name="planes_pool", bufs=2))
         work = ctx.enter_context(tc.tile_pool(name="work", bufs=4))
         a_pool = ctx.enter_context(tc.tile_pool(name="a_pool", bufs=3))
@@ -46,10 +46,9 @@ def tile_perception_pb_kernel(tc, msg, adj, b2, W3, out):
         small = ctx.enter_context(tc.tile_pool(name="small", bufs=2))
         d_pool = ctx.enter_context(tc.tile_pool(name="d_pool", bufs=6))
         out_pool = ctx.enter_context(tc.tile_pool(name="out_pool", bufs=4))
-        psum_acc = ctx.enter_context(tc.psum_pool(name="psum_acc", bufs=2))
+        psum_acc = ctx.enter_context(tc.psum_pool(name="psum_acc", bufs=3))
         psum_factor = ctx.enter_context(tc.psum_pool(name="psum_factor", bufs=3))
-        psum_misc = ctx.enter_context(tc.psum_pool(name="psum_misc", bufs=3))
-        ctx.enter_context(tc.manual_schedule())
+        psum_misc = ctx.enter_context(tc.psum_pool(name="psum_misc", bufs=2))
 
         def runs(ap, order):
             return ap.rearrange(order + " -> p c t i", i=RUN)
@@ -80,10 +79,6 @@ def tile_perception_pb_kernel(tc, msg, adj, b2, W3, out):
         make_identity(nc, ident_bf[:])
         b2_rows = keep.tile([P, P], BF16, name="b2_rows")
         nc.gpsimd.memset(b2_rows[:], 0.0)
-        left_cols = keep.tile([P, CHUNK_BLOCKS, P], BF16, name="left_cols")
-        nc.gpsimd.memset(left_cols[:], 0.0)
-        right_cols = keep.tile([P, CHUNK_BLOCKS, P], BF16, name="right_cols")
-        nc.gpsimd.memset(right_cols[:], 0.0)
         b2_col = keep.tile([P, PACK], F32, name="b2_col")
 
         def load_b2():
@@ -98,8 +93,6 @@ def tile_perception_pb_kernel(tc, msg, adj, b2, W3, out):
         sums = {}
         d_col = {}
         d_row = {}
-        left_rows = {}
-        right_rows = {}
 
         def load_chunk(b, q):
             chunk = adj_pool.tile([P, ROW_BLOCKS, CHUNK], BF16, name="chunk", tag="chunk")
@@ -157,35 +150,6 @@ def tile_perception_pb_kernel(tc, msg, adj, b2, W3, out):
             d_row[(b, q)] = d_pool.tile([P, CHUNK], F32, name="row", tag="row")
             nc.scalar.copy(out=d_row[(b, q)][:], in_=spread_ps[:])
 
-        def split(b, q):
-            d = d_col[(b, q)]
-            parts = small.tile([P, CHUNK_BLOCKS, PARTS], BF16, name="parts", tag="parts")
-            rest = small.tile(shape, F32, name="rest", tag="rest")
-            nc.gpsimd.tensor_copy(out=parts[:, :, 0], in_=d[:])
-            nc.gpsimd.tensor_tensor(out=rest[:], in0=d[:], in1=parts[:, :, 0], op=ALU.subtract)
-            nc.gpsimd.tensor_copy(out=parts[:, :, 1], in_=rest[:])
-            nc.gpsimd.tensor_tensor(out=parts[:, :, 2], in0=rest[:], in1=parts[:, :, 1], op=ALU.subtract)
-            for cols, axis in ((left_cols, 2), (right_cols, 3)):
-                nc.gpsimd.tensor_copy(
-                    out=cols[:, :, 0:PAIRS].rearrange("p k (a c) -> p k a c", a=PARTS),
-                    in_=parts[:].unsqueeze(axis).to_broadcast([P, CHUNK_BLOCKS, PARTS, PARTS]),
-                )
-
-        def turn_parts(b, q, cols, rows, tag):
-            rows_ps = psum_misc.tile([P, CHUNK], BF16, name="rows_ps", tag="misc")
-            for n in range(CHUNK_BLOCKS):
-                nc.tensor.transpose(
-                    out=rows_ps[:, n * P : (n + 1) * P], in_=cols[:, n, :], identity=ident_bf[:]
-                )
-            rows[(b, q)] = d_pool.tile([P, CHUNK], BF16, name=tag, tag=tag)
-            nc.scalar.copy(out=rows[(b, q)][:], in_=rows_ps[:])
-
-        def turn_left(b, q):
-            turn_parts(b, q, left_cols, left_rows, "left")
-
-        def turn_right(b, q):
-            turn_parts(b, q, right_cols, right_rows, "right")
-
         msg_codes = keep.tile([P, BATCH, PASSES, HIDDEN], U32, name="msg_codes", align_bytes=64)
         msg_scales = keep.tile([P, BATCH, PASSES, HIDDEN], U8, name="msg_scales", align_bytes=64)
         w3_codes = keep.tile([P, OUT_DIM], U32, name="w3_codes", align_bytes=64)
@@ -226,6 +190,7 @@ def tile_perception_pb_kernel(tc, msg, adj, b2, W3, out):
         last_chunk = len(chunks) - 1
 
         made = {}
+        complete = set()
         factors = {}
         a_grouped = {}
         a_codes = {}
@@ -239,14 +204,12 @@ def tile_perception_pb_kernel(tc, msg, adj, b2, W3, out):
 
         def kind(n, g):
             c = chunks[n][1] // CHUNK
-            if (n, g) == units[0]:
-                return "scalar"
-            if (c + g) % 2 == 0:
-                return "matmul"
-            return "scalar" if c < g else "mirror"
+            return "scalar" if c <= g else "mirror"
 
         def factor_by_scalar(n, g, ts):
             b, c = chunks[n][0], chunks[n][1] // CHUNK
+            if ts[-1] == PACK - 1:
+                complete.add((b, c, g))
             if ts[0] == 0:
                 made[(b, c, g)] = scaled_pool.tile([P, PACK, CHUNK], BF16, name="scaled", tag="scaled")
             planes = made[(b, c, g)]
@@ -266,15 +229,6 @@ def tile_perception_pb_kernel(tc, msg, adj, b2, W3, out):
             c, col = divmod(first_col + k * BANK_COLS, CHUNK)
             bank = psum_factor.tile([P, PACK, BANK_COLS], BF16, name="bank", tag="bank")
             for t in range(PACK):
-                if kind(n, g) == "matmul":
-                    nc.tensor.matmul(
-                        out=bank[:, t, :],
-                        lhsT=left_rows[(b, g)][:, t * P : (t + 1) * P],
-                        rhs=right_rows[(b, c)][:, col : col + BANK_COLS],
-                        start=True,
-                        stop=True,
-                    )
-                    continue
                 for m in range(BANK_COLS // P):
                     nc.tensor.transpose(
                         out=bank[:, t, m * P : (m + 1) * P],
@@ -389,28 +343,22 @@ def tile_perception_pb_kernel(tc, msg, adj, b2, W3, out):
         load_chunk(0, 0)
         load_chunk(0, 1)
         load_piece(0)
+        load_chunk(0, 2)
         load_piece(1)
         load_piece(2)
-        load_chunk(0, 2)
-        load_piece(3)
         load_chunk(0, 3)
+        load_piece(3)
         load_b2()
         load_chunk(1, 0)
 
         column_sums(0, 0, range(ROW_BLOCKS))
         degrees(0, 0, nc.vector)
         spread(0, 0)
-        split(0, 0)
         factor_by_scalar(*units[0], range(PACK))
         column_sums(0, 1, range(ROW_BLOCKS))
         degrees(0, 1, nc.vector)
         spread(0, 1)
         factor_by_scalar(*units[1], range(PACK))
-        turn_left(0, 0)
-        turn_right(0, 0)
-        split(0, 1)
-        turn_left(0, 1)
-        turn_right(0, 1)
 
         degree_steps = {
             (0, 2): (1, 2, 3, 3),
@@ -441,10 +389,8 @@ def tile_perception_pb_kernel(tc, msg, adj, b2, W3, out):
                 index, n, g, k = banks[0]
                 b, c = chunks[n][0], chunks[n][1] // CHUNK
                 if kind(n, g) == "mirror":
-                    if (b, g, c) not in made:
+                    if (b, g, c) not in complete:
                         return
-                elif (b, g) not in left_rows or (b, c) not in right_rows:
-                    return
                 factor_by_tensor(n, g, k)
                 banks.remove(banks[0])
                 pending += 1
@@ -455,7 +401,7 @@ def tile_perception_pb_kernel(tc, msg, adj, b2, W3, out):
                     load_chunk(1, q)
             for key, at in degree_steps.items():
                 if step == at[1]:
-                    degrees(*key, nc.gpsimd)
+                    degrees(*key, nc.vector)
             for n, at in regroups.items():
                 if step == at and n % 2 == 0:
                     regroup_piece(n, nc.vector.tensor_copy)
@@ -488,15 +434,10 @@ def tile_perception_pb_kernel(tc, msg, adj, b2, W3, out):
             for key, at in degree_steps.items():
                 if step == at[2]:
                     spread(*key)
-                if step == at[3]:
-                    turn_left(*key)
             make_banks(step, 1)
             for n, at in starts.items():
                 if 0 <= step - at - 6 < chunks[n][2] // P:
                     project(n, step - at - 6)
-            for key, at in degree_steps.items():
-                if step == at[3]:
-                    turn_right(*key)
             make_banks(step, 2)
             for n, at in starts.items():
                 if n < last_chunk and step == at:
@@ -511,9 +452,6 @@ def tile_perception_pb_kernel(tc, msg, adj, b2, W3, out):
             for key, at in degree_steps.items():
                 if step == at[0]:
                     column_sums(*key, range(ROW_BLOCKS))
-            for key, at in degree_steps.items():
-                if step == at[1]:
-                    split(*key)
             for n, at in regroups.items():
                 if step == at and n % 2 == 1:
                     regroup_piece(n, nc.scalar.copy)

@@ -45,6 +45,7 @@ def tile_perception_pb_kernel(tc, msg, adj, b2, W3, out):
         codes_pool = ctx.enter_context(tc.tile_pool(name="codes_pool", bufs=2))
         small = ctx.enter_context(tc.tile_pool(name="small", bufs=2))
         d_pool = ctx.enter_context(tc.tile_pool(name="d_pool", bufs=6))
+        row_pool = ctx.enter_context(tc.tile_pool(name="row_pool", bufs=CHUNKS))
         out_pool = ctx.enter_context(tc.tile_pool(name="out_pool", bufs=4))
         psum_acc = ctx.enter_context(tc.psum_pool(name="psum_acc", bufs=3))
         psum_factor = ctx.enter_context(tc.psum_pool(name="psum_factor", bufs=3))
@@ -79,6 +80,10 @@ def tile_perception_pb_kernel(tc, msg, adj, b2, W3, out):
         make_identity(nc, ident_bf[:])
         b2_rows = keep.tile([P, P], BF16, name="b2_rows")
         nc.gpsimd.memset(b2_rows[:], 0.0)
+        left_cols = keep.tile([P, CHUNK_BLOCKS, P], BF16, name="left_cols")
+        nc.gpsimd.memset(left_cols[:], 0.0)
+        right_cols = keep.tile([P, CHUNK_BLOCKS, P], BF16, name="right_cols")
+        nc.gpsimd.memset(right_cols[:], 0.0)
         b2_col = keep.tile([P, PACK], F32, name="b2_col")
 
         def load_b2():
@@ -92,6 +97,8 @@ def tile_perception_pb_kernel(tc, msg, adj, b2, W3, out):
         adj_chunks = {}
         sums = {}
         d_col = {}
+        left_rows = {}
+        right_rows = {}
         d_row = {}
 
         def load_chunk(b, q):
@@ -117,27 +124,53 @@ def tile_perception_pb_kernel(tc, msg, adj, b2, W3, out):
 
         shape = [P, CHUNK_BLOCKS]
 
-        def degrees(b, q, engine):
+        def degrees(b, q):
             c = small.tile(shape, F32, name="c", tag="c")
             nc.vector.tensor_reduce(out=c[:], in_=sums[(b, q)][:], axis=AXIS.X, op=ALU.add)
             c_floor = small.tile(shape, F32, name="c_floor", tag="c_floor")
-            engine.tensor_scalar_max(out=c_floor[:], in0=c[:], scalar1=1e-30)
+            nc.vector.tensor_scalar_max(out=c_floor[:], in0=c[:], scalar1=1e-30)
             guess = small.tile(shape, F32, name="guess", tag="guess")
             nc.scalar.activation(out=guess[:], in_=c_floor[:], func=ACT.Abs_reciprocal_sqrt)
-            positive = small.tile(shape, F32, name="positive", tag="positive")
-            engine.tensor_single_scalar(out=positive[:], in_=c[:], scalar=0.0, op=ALU.is_gt)
             square = small.tile(shape, F32, name="square", tag="square")
-            engine.tensor_mul(out=square[:], in0=guess[:], in1=guess[:])
-            product = small.tile(shape, F32, name="product", tag="product")
-            engine.tensor_mul(out=product[:], in0=square[:], in1=c_floor[:])
+            nc.vector.tensor_mul(out=square[:], in0=guess[:], in1=guess[:])
             masked = small.tile(shape, F32, name="masked", tag="masked")
-            engine.tensor_mul(out=masked[:], in0=guess[:], in1=positive[:])
+            nc.vector.scalar_tensor_tensor(
+                out=masked[:], in0=c[:], scalar=0.0, in1=guess[:], op0=ALU.is_gt, op1=ALU.mult
+            )
             newton = small.tile(shape, F32, name="newton", tag="newton")
-            engine.tensor_scalar(
-                out=newton[:], in0=product[:], scalar1=-0.5, scalar2=1.5, op0=ALU.mult, op1=ALU.add
+            nc.vector.scalar_tensor_tensor(
+                out=newton[:], in0=square[:], scalar=-0.5, in1=c_floor[:], op0=ALU.mult, op1=ALU.mult
             )
             d_col[(b, q)] = d_pool.tile(shape, F32, name="d", tag="d")
-            engine.tensor_mul(out=d_col[(b, q)][:], in0=newton[:], in1=masked[:])
+            nc.vector.scalar_tensor_tensor(
+                out=d_col[(b, q)][:], in0=newton[:], scalar=1.5, in1=masked[:], op0=ALU.add, op1=ALU.mult
+            )
+
+        parts = {}
+
+        def split(b, q):
+            d = d_col[(b, q)]
+            parts[(b, q)] = small.tile([P, CHUNK_BLOCKS, PARTS], BF16, name="parts", tag="parts")
+            split_into = parts[(b, q)]
+            rest = small.tile(shape, F32, name="rest", tag="rest")
+            nc.scalar.copy(out=split_into[:, :, 0], in_=d[:])
+            nc.vector.tensor_sub(out=rest[:], in0=d[:], in1=split_into[:, :, 0])
+            nc.scalar.copy(out=split_into[:, :, 1], in_=rest[:])
+            nc.vector.tensor_sub(out=split_into[:, :, 2], in0=rest[:], in1=split_into[:, :, 1])
+
+        def turn(b, q):
+            for cols, rows, axis in ((left_cols, left_rows, 2), (right_cols, right_rows, 3)):
+                nc.scalar.copy(
+                    out=cols[:, :, 0:PAIRS].rearrange("p k (a c) -> p k a c", a=PARTS),
+                    in_=parts[(b, q)][:].unsqueeze(axis).to_broadcast([P, CHUNK_BLOCKS, PARTS, PARTS]),
+                )
+                rows_ps = psum_misc.tile([P, CHUNK], BF16, name="rows_ps", tag="misc")
+                for n in range(CHUNK_BLOCKS):
+                    nc.tensor.transpose(
+                        out=rows_ps[:, n * P : (n + 1) * P], in_=cols[:, n, :], identity=ident_bf[:]
+                    )
+                rows[(b, q)] = row_pool.tile([P, CHUNK], BF16, name="rows%d" % axis, tag="rows%d" % axis)
+                nc.scalar.copy(out=rows[(b, q)][:], in_=rows_ps[:])
 
         def spread(b, q):
             spread_ps = psum_misc.tile([P, CHUNK], F32, name="spread_ps", tag="misc")
@@ -147,8 +180,11 @@ def tile_perception_pb_kernel(tc, msg, adj, b2, W3, out):
                     in_=d_col[(b, q)][:, n : n + 1].to_broadcast([P, P]),
                     identity=ident[:],
                 )
+            return spread_ps
+
+        def keep_row(b, q):
             d_row[(b, q)] = d_pool.tile([P, CHUNK], F32, name="row", tag="row")
-            nc.scalar.copy(out=d_row[(b, q)][:], in_=spread_ps[:])
+            nc.scalar.copy(out=d_row[(b, q)][:], in_=spread(b, q)[:])
 
         msg_codes = keep.tile([P, BATCH, PASSES, HIDDEN], U32, name="msg_codes", align_bytes=64)
         msg_scales = keep.tile([P, BATCH, PASSES, HIDDEN], U8, name="msg_scales", align_bytes=64)
@@ -203,7 +239,9 @@ def tile_perception_pb_kernel(tc, msg, adj, b2, W3, out):
         o_banks = {}
 
         def kind(n, g):
-            c = chunks[n][1] // CHUNK
+            b, c = chunks[n][0], chunks[n][1] // CHUNK
+            if b == BATCH - 1 and (n, g) != (4, 0):
+                return "matmul"
             return "scalar" if c <= g else "mirror"
 
         def factor_by_scalar(n, g, ts):
@@ -222,6 +260,19 @@ def tile_perception_pb_kernel(tc, msg, adj, b2, W3, out):
                     first = start % CHUNK
                     factors[(m, g)] = [planes[:, :, col : col + BANK_COLS] for col in range(first, first + width, BANK_COLS)]
 
+        def first_factor():
+            n, g = units[0]
+            made[(0, 0, 0)] = scaled_pool.tile([P, PACK, CHUNK], BF16, name="scaled", tag="scaled")
+            planes = made[(0, 0, 0)]
+            rows = [spread(0, 0), spread(0, 0)]
+            for t in range(PACK):
+                scale = d_col[(0, 0)][:, t : t + 1]
+                if t % 2 == 0:
+                    nc.scalar.activation(out=planes[:, t, :], in_=rows[0][:], func=ACT.Copy, scale=scale)
+                else:
+                    nc.vector.tensor_scalar_mul(out=planes[:, t, :], in0=rows[1][:], scalar1=scale)
+            factors[(n, g)] = [planes[:, :, col : col + BANK_COLS] for col in range(0, CHUNK, BANK_COLS)]
+
         def factor_by_tensor(n, g, k):
             b, first_col, width = chunks[n]
             if k * BANK_COLS >= width:
@@ -229,6 +280,15 @@ def tile_perception_pb_kernel(tc, msg, adj, b2, W3, out):
             c, col = divmod(first_col + k * BANK_COLS, CHUNK)
             bank = psum_factor.tile([P, PACK, BANK_COLS], BF16, name="bank", tag="bank")
             for t in range(PACK):
+                if kind(n, g) == "matmul":
+                    nc.tensor.matmul(
+                        out=bank[:, t, :],
+                        lhsT=left_rows[(b, g)][:, t * P : (t + 1) * P],
+                        rhs=right_rows[(b, c)][:, col : col + BANK_COLS],
+                        start=True,
+                        stop=True,
+                    )
+                    continue
                 for m in range(BANK_COLS // P):
                     nc.tensor.transpose(
                         out=bank[:, t, m * P : (m + 1) * P],
@@ -352,12 +412,12 @@ def tile_perception_pb_kernel(tc, msg, adj, b2, W3, out):
         load_chunk(1, 0)
 
         column_sums(0, 0, range(ROW_BLOCKS))
-        degrees(0, 0, nc.vector)
-        spread(0, 0)
-        factor_by_scalar(*units[0], range(PACK))
+        degrees(0, 0)
+        first_factor()
+        keep_row(0, 0)
         column_sums(0, 1, range(ROW_BLOCKS))
-        degrees(0, 1, nc.vector)
-        spread(0, 1)
+        degrees(0, 1)
+        keep_row(0, 1)
         factor_by_scalar(*units[1], range(PACK))
 
         degree_steps = {
@@ -391,6 +451,8 @@ def tile_perception_pb_kernel(tc, msg, adj, b2, W3, out):
                 if kind(n, g) == "mirror":
                     if (b, g, c) not in complete:
                         return
+                elif (b, g) not in left_rows or (b, c) not in right_rows:
+                    return
                 factor_by_tensor(n, g, k)
                 banks.remove(banks[0])
                 pending += 1
@@ -401,14 +463,14 @@ def tile_perception_pb_kernel(tc, msg, adj, b2, W3, out):
                     load_chunk(1, q)
             for key, at in degree_steps.items():
                 if step == at[1]:
-                    degrees(*key, nc.vector)
+                    degrees(*key)
             for n, at in regroups.items():
-                if step == at and n % 2 == 0:
+                if step == at and (n in (0, 2)):
                     regroup_piece(n, nc.vector.tensor_copy)
             if step < len(units):
                 scale(*units[step])
             for n, at in regroups.items():
-                if step == at + 1 + n % 2:
+                if step == at + 1 + (not (n in (0, 2))):
                     quantise_piece(n)
                     if n + RAW_BUFS < len(pieces):
                         load_piece(n + RAW_BUFS)
@@ -433,7 +495,12 @@ def tile_perception_pb_kernel(tc, msg, adj, b2, W3, out):
                         regroup_h(n, half)
             for key, at in degree_steps.items():
                 if step == at[2]:
-                    spread(*key)
+                    if key[0] == 0 or key[1] == 0:
+                        keep_row(*key)
+                    if key[0] == BATCH - 1:
+                        split(*key)
+                if step == at[2] + 1 and key[0] == BATCH - 1:
+                    turn(*key)
             make_banks(step, 1)
             for n, at in starts.items():
                 if 0 <= step - at - 6 < chunks[n][2] // P:
@@ -453,7 +520,7 @@ def tile_perception_pb_kernel(tc, msg, adj, b2, W3, out):
                 if step == at[0]:
                     column_sums(*key, range(ROW_BLOCKS))
             for n, at in regroups.items():
-                if step == at and n % 2 == 1:
+                if step == at and not (n in (0, 2)):
                     regroup_piece(n, nc.scalar.copy)
             emitted = 0
             for index, n, g, ts in waiting[:]:

@@ -213,7 +213,7 @@ def tile_perception_pb_kernel(tc, msg, adj, b2, W3, out):
         units = []
         for b in range(BATCH):
             first = len(chunks)
-            widths = [CHUNK] * 4 if b + 1 < BATCH else [CHUNK] * 3 + [CHUNK // 2] * 2
+            widths = [CHUNK] * 4 if b + 1 < BATCH else [CHUNK] * 2 + [CHUNK // 2] * 4
             col = 0
             for width in widths:
                 chunks.append((b, col, width))
@@ -277,14 +277,15 @@ def tile_perception_pb_kernel(tc, msg, adj, b2, W3, out):
             b, first_col, width = chunks[n]
             if k * BANK_COLS >= width:
                 return
+            cols = min(BANK_COLS, width)
             c, col = divmod(first_col + k * BANK_COLS, CHUNK)
-            bank = psum_factor.tile([P, PACK, BANK_COLS], BF16, name="bank", tag="bank")
+            bank = psum_factor.tile([P, PACK, cols], BF16, name="bank", tag="bank")
             for t in range(PACK):
                 if kind(n, g) == "matmul":
                     nc.tensor.matmul(
                         out=bank[:, t, :],
                         lhsT=left_rows[(b, g)][:, t * P : (t + 1) * P],
-                        rhs=right_rows[(b, c)][:, col : col + BANK_COLS],
+                        rhs=right_rows[(b, c)][:, col : col + cols],
                         start=True,
                         stop=True,
                     )
@@ -302,10 +303,10 @@ def tile_perception_pb_kernel(tc, msg, adj, b2, W3, out):
             c, local = divmod(first_col, CHUNK)
             grouped = work.tile([P, CHUNK, PACK], BF16, name="grouped", tag="grouped", align_bytes=64)
             rows = slice(g * PACK, (g + 1) * PACK)
-            for k in range(width // BANK_COLS):
-                cols = slice(local + k * BANK_COLS, local + (k + 1) * BANK_COLS)
+            for k in range(max(1, width // BANK_COLS)):
+                cols = slice(local + k * BANK_COLS, local + k * BANK_COLS + min(BANK_COLS, width))
                 nc.vector.tensor_tensor(
-                    out=runs(grouped[:, k * BANK_COLS : (k + 1) * BANK_COLS, :], "p (c i) t"),
+                    out=runs(grouped[:, k * BANK_COLS : k * BANK_COLS + min(BANK_COLS, width), :], "p (c i) t"),
                     in0=runs(adj_chunks[(b, c)][:, rows, cols], "p t (c i)"),
                     in1=runs(factors[(n, g)][k], "p t (c i)"),
                     op=ALU.mult,
@@ -380,7 +381,10 @@ def tile_perception_pb_kernel(tc, msg, adj, b2, W3, out):
         def project(n, it):
             b, first_col, width = chunks[n]
             i_cols = slice(it * P, (it + 1) * P)
-            o_ps = psum_misc.tile([P, OUT_DIM], F32, name="o_ps", tag="misc")
+            if n < last_chunk:
+                o_ps = psum_misc.tile([P, OUT_DIM], F32, name="o_ps", tag="misc")
+            else:
+                o_ps = psum_acc.tile([P, OUT_DIM], F32, name="o_ps", tag="acc")
             nc.tensor.matmul_mx(
                 out=o_ps[:],
                 lhsT=h_codes[n][:, i_cols].bitcast(FP8X4),
@@ -394,8 +398,11 @@ def tile_perception_pb_kernel(tc, msg, adj, b2, W3, out):
 
         def store(n, it):
             b, first_col, width = chunks[n]
-            o_sb = out_pool.tile([P, OUT_DIM], F32, name="o_sb", tag="o_sb")
-            copy = nc.vector.tensor_copy if n == last_chunk and it % 2 == 1 else nc.scalar.copy
+            if n + 1 < last_chunk:
+                o_sb = out_pool.tile([P, OUT_DIM], F32, name="o_sb", tag="o_sb")
+            else:
+                o_sb = raw_pool.tile([P, OUT_DIM], F32, name="o_sb", tag="raw")
+            copy = nc.vector.tensor_copy if n + 1 >= last_chunk and it % 2 == 1 else nc.scalar.copy
             copy(out=o_sb[:], in_=o_banks[(n, it)][:])
             first_row = first_col + it * P
             nc.sync.dma_start(out=out[b, first_row : first_row + P, :], in_=o_sb[:])
@@ -441,7 +448,7 @@ def tile_perception_pb_kernel(tc, msg, adj, b2, W3, out):
         banks = []
         for index, (n, g) in enumerate(units):
             if kind(n, g) != "scalar":
-                banks += [(index, n, g, k) for k in range(chunks[n][2] // BANK_COLS)]
+                banks += [(index, n, g, k) for k in range(max(1, chunks[n][2] // BANK_COLS))]
 
         def make_banks(step, limit):
             pending = len([1 for n, g in factors for bank in factors[(n, g)] if units.index((n, g)) > step and kind(n, g) != "scalar"])
@@ -486,10 +493,9 @@ def tile_perception_pb_kernel(tc, msg, adj, b2, W3, out):
                 if 0 <= step - at - 7 < chunks[n][2] // P:
                     store(n, step - at - 7)
             for n, at in starts.items():
-                if step == at + 1:
-                    relu(n, pairs[0])
-                if step == at + 2:
-                    relu(n, pairs[1])
+                for pair in pairs:
+                    if step == at + 1 + (pair[0] > 0 and n < last_chunk):
+                        relu(n, pair)
                 for half in range(2):
                     if step == at + 3 + half:
                         regroup_h(n, half)

@@ -47,8 +47,8 @@ def tile_perception_pb_kernel(tc, msg, adj, b2, W3, out):
         d_pool = ctx.enter_context(tc.tile_pool(name="d_pool", bufs=6))
         row_pool = ctx.enter_context(tc.tile_pool(name="row_pool", bufs=CHUNKS))
         out_pool = ctx.enter_context(tc.tile_pool(name="out_pool", bufs=4))
-        psum_acc = ctx.enter_context(tc.psum_pool(name="psum_acc", bufs=3))
-        psum_factor = ctx.enter_context(tc.psum_pool(name="psum_factor", bufs=3))
+        psum_acc = ctx.enter_context(tc.psum_pool(name="psum_acc", bufs=4))
+        psum_factor = ctx.enter_context(tc.psum_pool(name="psum_factor", bufs=2))
         psum_misc = ctx.enter_context(tc.psum_pool(name="psum_misc", bufs=2))
 
         def runs(ap, order):

@@ -72,6 +72,8 @@ def tile_perception_pb_kernel(tc, msg, adj, b2, W3, out):
         warm = keep.tile([P, 1], F32, name="warm")
         nc.vector.memset(warm[:], 1.0)
         nc.scalar.activation(out=warm[:], in_=warm[:], func=ACT.Abs_reciprocal_sqrt)
+        tiny = keep.tile([P, 1], F32, name="tiny")
+        nc.vector.memset(tiny[:], 1e-30)
         ones = keep.tile([P, 1], BF16, name="ones")
         nc.vector.memset(ones[:], 1.0)
         ident = keep.tile([P, P], F32, name="ident")
@@ -109,60 +111,63 @@ def tile_perception_pb_kernel(tc, msg, adj, b2, W3, out):
                 nc.sync.dma_start(out=chunk[:, blocks, :], in_=rows[:, blocks, q * CHUNK : (q + 1) * CHUNK])
             adj_chunks[(b, q)] = chunk
 
-        def column_sums(b, q, ks):
-            if ks[0] == 0:
-                sums[(b, q)] = psum_misc.tile([P, CHUNK_BLOCKS, ROW_BLOCKS], F32, name="sums", tag="misc")
-            for k in ks:
-                for n in range(CHUNK_BLOCKS):
-                    nc.tensor.matmul(
-                        out=sums[(b, q)][:, n, k : k + 1],
-                        lhsT=adj_chunks[(b, q)][:, k, n * P : (n + 1) * P],
-                        rhs=ones[:],
-                        start=True,
-                        stop=True,
-                    )
+        def column_sums(b, qs):
+            tile = psum_misc.tile([P, len(qs) * CHUNK_BLOCKS, ROW_BLOCKS], F32, name="sums", tag="misc")
+            for m, q in enumerate(qs):
+                for k in range(ROW_BLOCKS):
+                    for n in range(CHUNK_BLOCKS):
+                        nc.tensor.matmul(
+                            out=tile[:, m * CHUNK_BLOCKS + n, k : k + 1],
+                            lhsT=adj_chunks[(b, q)][:, k, n * P : (n + 1) * P],
+                            rhs=ones[:],
+                            start=True,
+                            stop=True,
+                        )
+            sums[(b, qs)] = tile
 
-        shape = [P, CHUNK_BLOCKS]
-
-        def degrees(b, q):
+        def degrees(b, qs):
+            shape = [P, len(qs) * CHUNK_BLOCKS]
             c = small.tile(shape, F32, name="c", tag="c")
-            nc.vector.tensor_reduce(out=c[:], in_=sums[(b, q)][:], axis=AXIS.X, op=ALU.add)
-            c_floor = small.tile(shape, F32, name="c_floor", tag="c_floor")
-            nc.vector.tensor_scalar_max(out=c_floor[:], in0=c[:], scalar1=1e-30)
+            nc.vector.tensor_reduce(out=c[:], in_=sums[(b, qs)][:], axis=AXIS.X, op=ALU.add)
             guess = small.tile(shape, F32, name="guess", tag="guess")
-            nc.scalar.activation(out=guess[:], in_=c_floor[:], func=ACT.Abs_reciprocal_sqrt)
+            nc.scalar.activation(out=guess[:], in_=c[:], func=ACT.Abs_reciprocal_sqrt, bias=tiny[:])
             square = small.tile(shape, F32, name="square", tag="square")
-            nc.vector.tensor_mul(out=square[:], in0=guess[:], in1=guess[:])
+            nc.scalar.activation(out=square[:], in_=guess[:], func=ACT.Square)
             masked = small.tile(shape, F32, name="masked", tag="masked")
             nc.vector.scalar_tensor_tensor(
                 out=masked[:], in0=c[:], scalar=0.0, in1=guess[:], op0=ALU.is_gt, op1=ALU.mult
             )
             newton = small.tile(shape, F32, name="newton", tag="newton")
             nc.vector.scalar_tensor_tensor(
-                out=newton[:], in0=square[:], scalar=-0.5, in1=c_floor[:], op0=ALU.mult, op1=ALU.mult
+                out=newton[:], in0=square[:], scalar=-0.5, in1=c[:], op0=ALU.mult, op1=ALU.mult
             )
-            d_col[(b, q)] = d_pool.tile(shape, F32, name="d", tag="d")
+            d = d_pool.tile(shape, F32, name="d", tag="d")
             nc.vector.scalar_tensor_tensor(
-                out=d_col[(b, q)][:], in0=newton[:], scalar=1.5, in1=masked[:], op0=ALU.add, op1=ALU.mult
+                out=d[:], in0=newton[:], scalar=1.5, in1=masked[:], op0=ALU.add, op1=ALU.mult
             )
+            for m, q in enumerate(qs):
+                d_col[(b, q)] = d[:, m * CHUNK_BLOCKS : (m + 1) * CHUNK_BLOCKS]
+            degree[(b, qs)] = d
 
+        degree = {}
         parts = {}
 
-        def split(b, q):
-            d = d_col[(b, q)]
-            parts[(b, q)] = small.tile([P, CHUNK_BLOCKS, PARTS], BF16, name="parts", tag="parts")
-            split_into = parts[(b, q)]
-            rest = small.tile(shape, F32, name="rest", tag="rest")
+        def split(b, qs):
+            d, blocks = degree[(b, qs)], len(qs) * CHUNK_BLOCKS
+            split_into = small.tile([P, blocks, PARTS], BF16, name="parts", tag="parts")
+            rest = small.tile([P, blocks], F32, name="rest", tag="rest")
             nc.scalar.copy(out=split_into[:, :, 0], in_=d[:])
             nc.vector.tensor_sub(out=rest[:], in0=d[:], in1=split_into[:, :, 0])
             nc.scalar.copy(out=split_into[:, :, 1], in_=rest[:])
             nc.vector.tensor_sub(out=split_into[:, :, 2], in0=rest[:], in1=split_into[:, :, 1])
+            for m, q in enumerate(qs):
+                parts[(b, q)] = split_into[:, m * CHUNK_BLOCKS : (m + 1) * CHUNK_BLOCKS, :]
 
         def turn(b, q):
             for cols, rows, axis in ((left_cols, left_rows, 2), (right_cols, right_rows, 3)):
                 nc.scalar.copy(
                     out=cols[:, :, 0:PAIRS].rearrange("p k (a c) -> p k a c", a=PARTS),
-                    in_=parts[(b, q)][:].unsqueeze(axis).to_broadcast([P, CHUNK_BLOCKS, PARTS, PARTS]),
+                    in_=parts[(b, q)].unsqueeze(axis).to_broadcast([P, CHUNK_BLOCKS, PARTS, PARTS]),
                 )
                 rows_ps = psum_misc.tile([P, CHUNK], BF16, name="rows_ps", tag="misc")
                 for n in range(CHUNK_BLOCKS):
@@ -418,22 +423,20 @@ def tile_perception_pb_kernel(tc, msg, adj, b2, W3, out):
         load_b2()
         load_chunk(1, 0)
 
-        column_sums(0, 0, range(ROW_BLOCKS))
-        degrees(0, 0)
+        column_sums(0, (0,))
+        degrees(0, (0,))
         first_factor()
         keep_row(0, 0)
-        column_sums(0, 1, range(ROW_BLOCKS))
-        degrees(0, 1)
+        column_sums(0, (1,))
+        degrees(0, (1,))
         keep_row(0, 1)
         factor_by_scalar(*units[1], range(PACK))
 
         degree_steps = {
-            (0, 2): (1, 2, 3, 3),
-            (0, 3): (2, 3, 4, 5),
-            (1, 0): (8, 10, 11, 13),
-            (1, 1): (11, 13, 14, 16),
-            (1, 2): (13, 16, 17, 19),
-            (1, 3): (16, 19, 20, 22),
+            (0, (2,)): (1, 2, 3, 3),
+            (0, (3,)): (2, 3, 4, 5),
+            (1, (0, 1)): (10, 11, 11, 12),
+            (1, (2, 3)): (14, 15, 15, 16),
         }
         regroups = {0: 0, 2: 1, 1: 1, 3: 2, 4: 4, 5: 6, 6: 8, 7: 10, 8: 12}
         AHEAD = 5
@@ -501,12 +504,14 @@ def tile_perception_pb_kernel(tc, msg, adj, b2, W3, out):
                         regroup_h(n, half)
             for key, at in degree_steps.items():
                 if step == at[2]:
-                    if key[0] == 0 or key[1] == 0:
-                        keep_row(*key)
+                    for q in key[1]:
+                        if key[0] == 0 or q == 0:
+                            keep_row(key[0], q)
                     if key[0] == BATCH - 1:
                         split(*key)
-                if step == at[2] + 1 and key[0] == BATCH - 1:
-                    turn(*key)
+                if step == at[3] and key[0] == BATCH - 1:
+                    for q in key[1]:
+                        turn(key[0], q)
             make_banks(step, 1)
             for n, at in starts.items():
                 if 0 <= step - at - 6 < chunks[n][2] // P:
@@ -524,7 +529,7 @@ def tile_perception_pb_kernel(tc, msg, adj, b2, W3, out):
             make_banks(step, 3)
             for key, at in degree_steps.items():
                 if step == at[0]:
-                    column_sums(*key, range(ROW_BLOCKS))
+                    column_sums(*key)
             for n, at in regroups.items():
                 if step == at and not (n in (0, 2)):
                     regroup_piece(n, nc.scalar.copy)

@@ -233,6 +233,7 @@ def tile_perception_pb_kernel(tc, msg, adj, b2, W3, out):
         made = {}
         complete = set()
         factors = {}
+        a_planes = {}
         a_grouped = {}
         a_codes = {}
         a_scales = {}
@@ -303,11 +304,23 @@ def tile_perception_pb_kernel(tc, msg, adj, b2, W3, out):
                     )
             factors.setdefault((n, g), []).append(bank)
 
+        def on_planes(n, g):
+            return kind(n, g) == "matmul" and (n in (4, 5) and g == 3)
+
         def scale(n, g):
             b, first_col, width = chunks[n]
             c, local = divmod(first_col, CHUNK)
-            grouped = work.tile([P, CHUNK, PACK], BF16, name="grouped", tag="grouped", align_bytes=64)
             rows = slice(g * PACK, (g + 1) * PACK)
+            if on_planes(n, g):
+                a_planes[(n, g)] = scaled_pool.tile([P, PACK, CHUNK], BF16, name="scaled", tag="scaled")
+                for k in range(width // BANK_COLS):
+                    nc.vector.tensor_mul(
+                        out=a_planes[(n, g)][:, :, k * BANK_COLS : (k + 1) * BANK_COLS],
+                        in0=adj_chunks[(b, c)][:, rows, local + k * BANK_COLS : local + (k + 1) * BANK_COLS],
+                        in1=factors[(n, g)][k][:],
+                    )
+                return
+            grouped = work.tile([P, CHUNK, PACK], BF16, name="grouped", tag="grouped", align_bytes=64)
             for k in range(max(1, width // BANK_COLS)):
                 cols = slice(local + k * BANK_COLS, local + k * BANK_COLS + min(BANK_COLS, width))
                 nc.vector.tensor_tensor(
@@ -447,6 +460,7 @@ def tile_perception_pb_kernel(tc, msg, adj, b2, W3, out):
                 waiting += [(index, *units[index], range(0, 2)), (index, *units[index], range(2, 4))]
         TAIL = 1
         starts = {}
+        quantised = [0] * len(chunks)
         pairs = ((0, 1), (2, 3))
         banks = []
         for index, (n, g) in enumerate(units):
@@ -484,11 +498,13 @@ def tile_perception_pb_kernel(tc, msg, adj, b2, W3, out):
                     quantise_piece(n)
                     if n + RAW_BUFS < len(pieces):
                         load_piece(n + RAW_BUFS)
-            if 0 <= step - 1 < len(units):
-                n, g = units[step - 1]
-                quantise_a(n, g)
-                if g == PASSES - 1:
-                    starts[n] = max(step + 1, starts[n - 1] + 3) if n > 0 else step + 1
+            for lag in (3, 1):
+                if 0 <= step - lag < len(units) and on_planes(*units[step - lag]) == (lag == 3):
+                    n, g = units[step - lag]
+                    quantise_a(n, g)
+                    quantised[n] += 1
+                    if quantised[n] == PASSES:
+                        starts[n] = max(step + 1, starts[n - 1] + 3) if n > 0 else step + 1
             for n, at in starts.items():
                 if step == at + 5:
                     quantise_h(n)
@@ -520,7 +536,7 @@ def tile_perception_pb_kernel(tc, msg, adj, b2, W3, out):
             for n, at in starts.items():
                 if n < last_chunk and step == at:
                     aggregate(n, pairs[0], range(PASSES))
-                if n < last_chunk and step == at + 1:
+                if n < last_chunk and step == at:
                     aggregate(n, pairs[1], range(PASSES))
             if step >= len(units) - PASSES + 2 and step < len(units) + 2:
                 g = step - (len(units) - PASSES + 2)
@@ -530,6 +546,9 @@ def tile_perception_pb_kernel(tc, msg, adj, b2, W3, out):
             for key, at in degree_steps.items():
                 if step == at[0]:
                     column_sums(*key)
+            if step < len(units) and on_planes(*units[step]):
+                n, g = units[step]
+                a_grouped[(n, g)] = regroup(nc.scalar.copy, a_planes[(n, g)], chunks[n][2])
             for n, at in regroups.items():
                 if step == at and not (n in (0, 2)):
                     regroup_piece(n, nc.scalar.copy)

@@ -106,8 +106,9 @@ def tile_perception_pb_kernel(tc, msg, adj, b2, W3, out):
         def load_chunk(b, q):
             chunk = adj_pool.tile([P, ROW_BLOCKS, CHUNK], BF16, name="chunk", tag="chunk")
             rows = adj[b].rearrange("(k p) i -> p k i", p=P)
-            for first in range(0, ROW_BLOCKS, LOAD_BLOCKS):
-                blocks = slice(first, first + LOAD_BLOCKS)
+            load_blocks = 2 if (b, q) == (0, 0) else LOAD_BLOCKS
+            for first in range(0, ROW_BLOCKS, load_blocks):
+                blocks = slice(first, first + load_blocks)
                 nc.sync.dma_start(out=chunk[:, blocks, :], in_=rows[:, blocks, q * CHUNK : (q + 1) * CHUNK])
             adj_chunks[(b, q)] = chunk
 
@@ -383,7 +384,7 @@ def tile_perception_pb_kernel(tc, msg, adj, b2, W3, out):
 
         def regroup_h(n, half):
             copy = nc.vector.tensor_copy if n >= last_chunk - TAIL else nc.scalar.copy
-            cols = slice(half * chunks[n][2] // 2, (half + 1) * chunks[n][2] // 2)
+            cols = slice(half * BANK_COLS, (half + 1) * BANK_COLS)
             if half == 0:
                 h_grouped[n] = planes_pool.tile(
                     [P, CHUNK, PACK], BF16, name="h_grouped", tag="h_grouped", align_bytes=64
@@ -489,12 +490,12 @@ def tile_perception_pb_kernel(tc, msg, adj, b2, W3, out):
                 if step == at[1]:
                     degrees(*key)
             for n, at in regroups.items():
-                if step == at and (n in (0, 2)):
+                if step == at and (n == 2):
                     regroup_piece(n, nc.vector.tensor_copy)
             if step < len(units):
                 scale(*units[step])
             for n, at in regroups.items():
-                if step == at + 1 + (not (n in (0, 2))):
+                if step == at + 1 + (not (n == 2)):
                     quantise_piece(n)
                     if n + RAW_BUFS < len(pieces):
                         load_piece(n + RAW_BUFS)
@@ -515,7 +516,7 @@ def tile_perception_pb_kernel(tc, msg, adj, b2, W3, out):
                 for pair in pairs:
                     if step == at + 1 + (pair[0] > 0 and n < last_chunk):
                         relu(n, pair)
-                for half in range(2):
+                for half in range(chunks[n][2] // BANK_COLS):
                     if step == at + 3 + half:
                         regroup_h(n, half)
             for key, at in degree_steps.items():
@@ -550,7 +551,7 @@ def tile_perception_pb_kernel(tc, msg, adj, b2, W3, out):
                 n, g = units[step]
                 a_grouped[(n, g)] = regroup(nc.scalar.copy, a_planes[(n, g)], chunks[n][2])
             for n, at in regroups.items():
-                if step == at and not (n in (0, 2)):
+                if step == at and not (n == 2):
                     regroup_piece(n, nc.scalar.copy)
             emitted = 0
             for index, n, g, ts in waiting[:]:

from contextlib import ExitStack

import concourse.mybir as mybir
from concourse.masks import make_identity

F32 = mybir.dt.float32
BF16 = mybir.dt.bfloat16
U32 = mybir.dt.uint32
U8 = mybir.dt.uint8
FP8X4 = mybir.dt.float8_e4m3fn_x4
ALU = mybir.AluOpType
ACT = mybir.ActivationFunctionType
AXIS = mybir.AxisListType

BATCH, NODES, HIDDEN, OUT_DIM = 2, 2048, 512, 512
FLOPS = 2 * BATCH * NODES * NODES * HIDDEN + 2 * BATCH * NODES * HIDDEN * OUT_DIM

P = 128
PACK = 4
K_PASS = P * PACK
PASSES = NODES // K_PASS
ROW_BLOCKS = NODES // P
CHUNK = 512
CHUNKS = NODES // CHUNK
CHUNK_BLOCKS = CHUNK // P
F_TILES = HIDDEN // P
RUN = 4
LOAD_BLOCKS = 4
PARTS = 3
PAIRS = PARTS * PARTS
BANK_COLS = 256
RAW_BUFS = 4


def tile_perception_pb_kernel(tc, msg, adj, b2, W3, out):
    nc = tc.nc
    with ExitStack() as ctx:
        keep = ctx.enter_context(tc.tile_pool(name="keep", bufs=1))
        adj_pool = ctx.enter_context(tc.tile_pool(name="adj_pool", bufs=5))
        raw_pool = ctx.enter_context(tc.tile_pool(name="raw_pool", bufs=RAW_BUFS))
        scaled_pool = ctx.enter_context(tc.tile_pool(name="scaled_pool", bufs=5))
        planes_pool = ctx.enter_context(tc.tile_pool(name="planes_pool", bufs=2))
        work = ctx.enter_context(tc.tile_pool(name="work", bufs=4))
        a_pool = ctx.enter_context(tc.tile_pool(name="a_pool", bufs=3))
        codes_pool = ctx.enter_context(tc.tile_pool(name="codes_pool", bufs=2))
        small = ctx.enter_context(tc.tile_pool(name="small", bufs=2))
        d_pool = ctx.enter_context(tc.tile_pool(name="d_pool", bufs=6))
        row_pool = ctx.enter_context(tc.tile_pool(name="row_pool", bufs=CHUNKS))
        out_pool = ctx.enter_context(tc.tile_pool(name="out_pool", bufs=4))
        psum_acc = ctx.enter_context(tc.psum_pool(name="psum_acc", bufs=4))
        psum_factor = ctx.enter_context(tc.psum_pool(name="psum_factor", bufs=2))
        psum_misc = ctx.enter_context(tc.psum_pool(name="psum_misc", bufs=2))

        def runs(ap, order):
            return ap.rearrange(order + " -> p c t i", i=RUN)

        def regroup(copy, planes, width):
            grouped = work.tile([P, CHUNK, PACK], BF16, name="grouped", tag="grouped", align_bytes=64)
            copy(
                out=runs(grouped[:, 0:width, :], "p (c i) t"),
                in_=runs(planes[:, :, 0:width], "p t (c i)"),
            )
            return grouped

        def quantise(grouped, codes, scales, width):
            nc.vector.quantize_mx(
                out=codes.bitcast(FP8X4),
                scales=scales,
                in_=grouped[:, 0:width, :].rearrange("p w t -> p (w t)"),
            )

        warm = keep.tile([P, 1], F32, name="warm")
        nc.vector.memset(warm[:], 1.0)
        nc.scalar.activation(out=warm[:], in_=warm[:], func=ACT.Abs_reciprocal_sqrt)
        tiny = keep.tile([P, 1], F32, name="tiny")
        nc.vector.memset(tiny[:], 1e-30)
        ones = keep.tile([P, 1], BF16, name="ones")
        nc.vector.memset(ones[:], 1.0)
        ident = keep.tile([P, P], F32, name="ident")
        make_identity(nc, ident[:])
        ident_bf = keep.tile([P, P], BF16, name="ident_bf")
        make_identity(nc, ident_bf[:])
        b2_rows = keep.tile([P, P], BF16, name="b2_rows")
        nc.gpsimd.memset(b2_rows[:], 0.0)
        left_cols = keep.tile([P, CHUNK_BLOCKS, P], BF16, name="left_cols")
        nc.gpsimd.memset(left_cols[:], 0.0)
        right_cols = keep.tile([P, CHUNK_BLOCKS, P], BF16, name="right_cols")
        nc.gpsimd.memset(right_cols[:], 0.0)
        b2_col = keep.tile([P, PACK], F32, name="b2_col")

        def load_b2():
            nc.sync.dma_start(out=b2_rows[0:PACK, :], in_=b2.rearrange("(t p) -> t p", p=P))

        def turn_b2():
            b2_ps = psum_misc.tile([P, P], BF16, name="b2_ps", tag="misc")
            nc.tensor.transpose(out=b2_ps[:], in_=b2_rows[:], identity=ident_bf[:])
            nc.scalar.copy(out=b2_col[:], in_=b2_ps[:, 0:PACK])

        adj_chunks = {}
        sums = {}
        d_col = {}
        left_rows = {}
        right_rows = {}
        d_row = {}

        def load_chunk(b, q):
            chunk = adj_pool.tile([P, ROW_BLOCKS, CHUNK], BF16, name="chunk", tag="chunk")
            rows = adj[b].rearrange("(k p) i -> p k i", p=P)
            load_blocks = 2 if (b, q) == (0, 0) else LOAD_BLOCKS
            for first in range(0, ROW_BLOCKS, load_blocks):
                blocks = slice(first, first + load_blocks)
                nc.sync.dma_start(out=chunk[:, blocks, :], in_=rows[:, blocks, q * CHUNK : (q + 1) * CHUNK])
            adj_chunks[(b, q)] = chunk

        def column_sums(b, qs):
            tile = psum_misc.tile([P, len(qs) * CHUNK_BLOCKS, ROW_BLOCKS], F32, name="sums", tag="misc")
            for m, q in enumerate(qs):
                for k in range(ROW_BLOCKS):
                    for n in range(CHUNK_BLOCKS):
                        nc.tensor.matmul(
                            out=tile[:, m * CHUNK_BLOCKS + n, k : k + 1],
                            lhsT=adj_chunks[(b, q)][:, k, n * P : (n + 1) * P],
                            rhs=ones[:],
                            start=True,
                            stop=True,
                        )
            sums[(b, qs)] = tile

        def degrees(b, qs):
            shape = [P, len(qs) * CHUNK_BLOCKS]
            c = small.tile(shape, F32, name="c", tag="c")
            nc.vector.tensor_reduce(out=c[:], in_=sums[(b, qs)][:], axis=AXIS.X, op=ALU.add)
            guess = small.tile(shape, F32, name="guess", tag="guess")
            nc.scalar.activation(out=guess[:], in_=c[:], func=ACT.Abs_reciprocal_sqrt, bias=tiny[:])
            square = small.tile(shape, F32, name="square", tag="square")
            nc.scalar.activation(out=square[:], in_=guess[:], func=ACT.Square)
            masked = small.tile(shape, F32, name="masked", tag="masked")
            nc.vector.scalar_tensor_tensor(
                out=masked[:], in0=c[:], scalar=0.0, in1=guess[:], op0=ALU.is_gt, op1=ALU.mult
            )
            newton = small.tile(shape, F32, name="newton", tag="newton")
            nc.vector.scalar_tensor_tensor(
                out=newton[:], in0=square[:], scalar=-0.5, in1=c[:], op0=ALU.mult, op1=ALU.mult
            )
            d = d_pool.tile(shape, F32, name="d", tag="d")
            nc.vector.scalar_tensor_tensor(
                out=d[:], in0=newton[:], scalar=1.5, in1=masked[:], op0=ALU.add, op1=ALU.mult
            )
            for m, q in enumerate(qs):
                d_col[(b, q)] = d[:, m * CHUNK_BLOCKS : (m + 1) * CHUNK_BLOCKS]
            degree[(b, qs)] = d

        degree = {}
        parts = {}

        def split(b, qs):
            d, blocks = degree[(b, qs)], len(qs) * CHUNK_BLOCKS
            split_into = small.tile([P, blocks, PARTS], BF16, name="parts", tag="parts")
            rest = small.tile([P, blocks], F32, name="rest", tag="rest")
            nc.scalar.copy(out=split_into[:, :, 0], in_=d[:])
            nc.vector.tensor_sub(out=rest[:], in0=d[:], in1=split_into[:, :, 0])
            nc.scalar.copy(out=split_into[:, :, 1], in_=rest[:])
            nc.vector.tensor_sub(out=split_into[:, :, 2], in0=rest[:], in1=split_into[:, :, 1])
            for m, q in enumerate(qs):
                parts[(b, q)] = split_into[:, m * CHUNK_BLOCKS : (m + 1) * CHUNK_BLOCKS, :]

        def turn(b, q):
            for cols, rows, axis in ((left_cols, left_rows, 2), (right_cols, right_rows, 3)):
                nc.scalar.copy(
                    out=cols[:, :, 0:PAIRS].rearrange("p k (a c) -> p k a c", a=PARTS),
                    in_=parts[(b, q)].unsqueeze(axis).to_broadcast([P, CHUNK_BLOCKS, PARTS, PARTS]),
                )
                rows_ps = psum_misc.tile([P, CHUNK], BF16, name="rows_ps", tag="misc")
                for n in range(CHUNK_BLOCKS):
                    nc.tensor.transpose(
                        out=rows_ps[:, n * P : (n + 1) * P], in_=cols[:, n, :], identity=ident_bf[:]
                    )
                rows[(b, q)] = row_pool.tile([P, CHUNK], BF16, name="rows%d" % axis, tag="rows%d" % axis)
                nc.scalar.copy(out=rows[(b, q)][:], in_=rows_ps[:])

        def spread(b, q):
            spread_ps = psum_misc.tile([P, CHUNK], F32, name="spread_ps", tag="misc")
            for n in range(CHUNK_BLOCKS):
                nc.tensor.transpose(
                    out=spread_ps[:, n * P : (n + 1) * P],
                    in_=d_col[(b, q)][:, n : n + 1].to_broadcast([P, P]),
                    identity=ident[:],
                )
            return spread_ps

        def keep_row(b, q):
            d_row[(b, q)] = d_pool.tile([P, CHUNK], F32, name="row", tag="row")
            nc.scalar.copy(out=d_row[(b, q)][:], in_=spread(b, q)[:])

        msg_codes = keep.tile([P, BATCH, PASSES, HIDDEN], U32, name="msg_codes", align_bytes=64)
        msg_scales = keep.tile([P, BATCH, PASSES, HIDDEN], U8, name="msg_scales", align_bytes=64)
        w3_codes = keep.tile([P, OUT_DIM], U32, name="w3_codes", align_bytes=64)
        w3_scales = keep.tile([P, OUT_DIM], U8, name="w3_scales", align_bytes=64)
        w3_piece = (W3.rearrange("(t p) d -> p t d", p=P), w3_codes[:], w3_scales[:])
        msg_pieces = []
        for b in range(BATCH):
            rows = msg[b].rearrange("(g t p) f -> g p t f", t=PACK, p=P)
            msg_pieces.append([(rows[g], msg_codes[:, b, g, :], msg_scales[:, b, g, :]) for g in range(PASSES)])
        pieces = msg_pieces[0] + [w3_piece] + msg_pieces[1]
        raws = {}
        piece_grouped = {}

        def load_piece(n):
            raws[n] = raw_pool.tile([P, PACK, CHUNK], BF16, name="raw", tag="raw")
            nc.sync.dma_start(out=raws[n][:], in_=pieces[n][0])

        def regroup_piece(n, copy):
            piece_grouped[n] = regroup(copy, raws[n], CHUNK)

        def quantise_piece(n):
            quantise(piece_grouped[n], pieces[n][1], pieces[n][2], CHUNK)

        chunks = []
        units = []
        for b in range(BATCH):
            first = len(chunks)
            widths = [CHUNK] * 4 if b + 1 < BATCH else [CHUNK] * 2 + [CHUNK // 2] * 4
            col = 0
            for width in widths:
                chunks.append((b, col, width))
                col += width
            for gs in ((0, 1), (2,), (3,)):
                for n in (first, first + 1):
                    units += [(n, g) for g in gs]
            for n in range(first + 2, len(chunks)):
                units += [(n, g) for g in range(PASSES)]
        last_chunk = len(chunks) - 1

        made = {}
        complete = set()
        factors = {}
        a_planes = {}
        a_grouped = {}
        a_codes = {}
        a_scales = {}
        acc = {}
        h_planes = {}
        h_grouped = {}
        h_codes = {}
        h_scales = {}
        o_banks = {}

        def kind(n, g):
            b, c = chunks[n][0], chunks[n][1] // CHUNK
            if b == BATCH - 1 and (n, g) != (4, 0):
                return "matmul"
            return "scalar" if c <= g else "mirror"

        def factor_by_scalar(n, g, ts):
            b, c = chunks[n][0], chunks[n][1] // CHUNK
            if ts[-1] == PACK - 1:
                complete.add((b, c, g))
            if ts[0] == 0:
                made[(b, c, g)] = scaled_pool.tile([P, PACK, CHUNK], BF16, name="scaled", tag="scaled")
            planes = made[(b, c, g)]
            for t in ts:
                nc.scalar.activation(
                    out=planes[:, t, :], in_=d_row[(b, c)][:], func=ACT.Copy, scale=d_col[(b, g)][:, t : t + 1]
                )
            for m, (batch, start, width) in enumerate(chunks):
                if batch == b and start // CHUNK == c:
                    first = start % CHUNK
                    factors[(m, g)] = [planes[:, :, col : col + BANK_COLS] for col in range(first, first + width, BANK_COLS)]

        def first_factor():
            n, g = units[0]
            made[(0, 0, 0)] = scaled_pool.tile([P, PACK, CHUNK], BF16, name="scaled", tag="scaled")
            planes = made[(0, 0, 0)]
            rows = [spread(0, 0), spread(0, 0)]
            for t in range(PACK):
                scale = d_col[(0, 0)][:, t : t + 1]
                if t % 2 == 0:
                    nc.scalar.activation(out=planes[:, t, :], in_=rows[0][:], func=ACT.Copy, scale=scale)
                else:
                    nc.vector.tensor_scalar_mul(out=planes[:, t, :], in0=rows[1][:], scalar1=scale)
            factors[(n, g)] = [planes[:, :, col : col + BANK_COLS] for col in range(0, CHUNK, BANK_COLS)]

        def factor_by_tensor(n, g, k):
            b, first_col, width = chunks[n]
            if k * BANK_COLS >= width:
                return
            cols = min(BANK_COLS, width)
            c, col = divmod(first_col + k * BANK_COLS, CHUNK)
            bank = psum_factor.tile([P, PACK, cols], BF16, name="bank", tag="bank")
            for t in range(PACK):
                if kind(n, g) == "matmul":
                    nc.tensor.matmul(
                        out=bank[:, t, :],
                        lhsT=left_rows[(b, g)][:, t * P : (t + 1) * P],
                        rhs=right_rows[(b, c)][:, col : col + cols],
                        start=True,
                        stop=True,
                    )
                    continue
                for m in range(BANK_COLS // P):
                    nc.tensor.transpose(
                        out=bank[:, t, m * P : (m + 1) * P],
                        in_=made[(b, g, c)][:, col // P + m, t * P : (t + 1) * P],
                        identity=ident_bf[:],
                    )
            factors.setdefault((n, g), []).append(bank)

        def on_planes(n, g):
            return kind(n, g) == "matmul" and (n in (4, 5) and g == 3)

        def scale(n, g):
            b, first_col, width = chunks[n]
            c, local = divmod(first_col, CHUNK)
            rows = slice(g * PACK, (g + 1) * PACK)
            if on_planes(n, g):
                a_planes[(n, g)] = scaled_pool.tile([P, PACK, CHUNK], BF16, name="scaled", tag="scaled")
                for k in range(width // BANK_COLS):
                    nc.vector.tensor_mul(
                        out=a_planes[(n, g)][:, :, k * BANK_COLS : (k + 1) * BANK_COLS],
                        in0=adj_chunks[(b, c)][:, rows, local + k * BANK_COLS : local + (k + 1) * BANK_COLS],
                        in1=factors[(n, g)][k][:],
                    )
                return
            grouped = work.tile([P, CHUNK, PACK], BF16, name="grouped", tag="grouped", align_bytes=64)
            for k in range(max(1, width // BANK_COLS)):
                cols = slice(local + k * BANK_COLS, local + k * BANK_COLS + min(BANK_COLS, width))
                nc.vector.tensor_tensor(
                    out=runs(grouped[:, k * BANK_COLS : k * BANK_COLS + min(BANK_COLS, width), :], "p (c i) t"),
                    in0=runs(adj_chunks[(b, c)][:, rows, cols], "p t (c i)"),
                    in1=runs(factors[(n, g)][k], "p t (c i)"),
                    op=ALU.mult,
                )
            a_grouped[(n, g)] = grouped

        def quantise_a(n, g):
            width = chunks[n][2]
            if n not in a_codes:
                a_codes[n] = a_pool.tile([P, PASSES, CHUNK], U32, name="a_codes", tag="a_codes", align_bytes=64)
                a_scales[n] = a_pool.tile([P, PASSES, CHUNK], U8, name="a_scales", tag="a_scales", align_bytes=64)
            quantise(a_grouped[(n, g)], a_codes[n][:, g, 0:width], a_scales[n][:, g, 0:width], width)

        def aggregate(n, pair, passes):
            b, first_col, width = chunks[n]
            for ft in pair:
                if passes[0] == 0 and n == last_chunk and ft >= 2:
                    acc[(n, ft)] = psum_factor.tile([P, CHUNK], F32, name="acc", tag="bank")
                elif passes[0] == 0:
                    acc[(n, ft)] = psum_acc.tile([P, CHUNK], F32, name="acc", tag="acc")
            for g in passes:
                for ft in pair:
                    f_cols = slice(ft * P, (ft + 1) * P)
                    nc.tensor.matmul_mx(
                        out=acc[(n, ft)][:, 0:width],
                        lhsT=msg_codes[:, b, g, f_cols].bitcast(FP8X4),
                        lhsT_scale=msg_scales[:, b, g, f_cols],
                        rhs=a_codes[n][:, g, 0:width].bitcast(FP8X4),
                        rhs_scale=a_scales[n][:, g, 0:width],
                        start=(g == 0),
                        stop=(g == PASSES - 1),
                    )

        def relu(n, pair):
            width = chunks[n][2]
            if pair[0] == 0:
                h_planes[n] = planes_pool.tile([P, PACK, CHUNK], BF16, name="h_planes", tag="planes")
            for ft in pair:
                if n == last_chunk and ft % 2 == 1:
                    nc.vector.tensor_scalar(
                        out=h_planes[n][:, ft, 0:width],
                        in0=acc[(n, ft)][:, 0:width],
                        scalar1=b2_col[:, ft : ft + 1],
                        scalar2=0.0,
                        op0=ALU.add,
                        op1=ALU.max,
                    )
                else:
                    nc.scalar.activation(
                        out=h_planes[n][:, ft, 0:width],
                        in_=acc[(n, ft)][:, 0:width],
                        func=ACT.Relu,
                        bias=b2_col[:, ft : ft + 1],
                        scale=1.0,
                    )

        def regroup_h(n, half):
            copy = nc.vector.tensor_copy if n >= last_chunk - TAIL else nc.scalar.copy
            cols = slice(half * BANK_COLS, (half + 1) * BANK_COLS)
            if half == 0:
                h_grouped[n] = planes_pool.tile(
                    [P, CHUNK, PACK], BF16, name="h_grouped", tag="h_grouped", align_bytes=64
                )
            copy(out=runs(h_grouped[n][:, cols, :], "p (c i) t"), in_=runs(h_planes[n][:, :, cols], "p t (c i)"))

        def quantise_h(n):
            width = chunks[n][2]
            h_codes[n] = codes_pool.tile([P, CHUNK], U32, name="h_codes", tag="h_codes", align_bytes=64)
            h_scales[n] = codes_pool.tile([P, CHUNK], U8, name="h_scales", tag="h_scales", align_bytes=64)
            quantise(h_grouped[n], h_codes[n][:, 0:width], h_scales[n][:, 0:width], width)

        def project(n, it):
            b, first_col, width = chunks[n]
            i_cols = slice(it * P, (it + 1) * P)
            if n < last_chunk:
                o_ps = psum_misc.tile([P, OUT_DIM], F32, name="o_ps", tag="misc")
            else:
                o_ps = psum_acc.tile([P, OUT_DIM], F32, name="o_ps", tag="acc")
            nc.tensor.matmul_mx(
                out=o_ps[:],
                lhsT=h_codes[n][:, i_cols].bitcast(FP8X4),
                lhsT_scale=h_scales[n][:, i_cols],
                rhs=w3_codes[:].bitcast(FP8X4),
                rhs_scale=w3_scales[:],
                start=True,
                stop=True,
            )
            o_banks[(n, it)] = o_ps

        def store(n, it):
            b, first_col, width = chunks[n]
            if n + 1 < last_chunk:
                o_sb = out_pool.tile([P, OUT_DIM], F32, name="o_sb", tag="o_sb")
            else:
                o_sb = raw_pool.tile([P, OUT_DIM], F32, name="o_sb", tag="raw")
            copy = nc.vector.tensor_copy if n + 1 >= last_chunk and it % 2 == 1 else nc.scalar.copy
            copy(out=o_sb[:], in_=o_banks[(n, it)][:])
            first_row = first_col + it * P
            nc.sync.dma_start(out=out[b, first_row : first_row + P, :], in_=o_sb[:])

        load_chunk(0, 0)
        load_chunk(0, 1)
        load_piece(0)
        load_chunk(0, 2)
        load_piece(1)
        load_piece(2)
        load_chunk(0, 3)
        load_piece(3)
        load_b2()
        load_chunk(1, 0)

        column_sums(0, (0,))
        degrees(0, (0,))
        first_factor()
        keep_row(0, 0)
        column_sums(0, (1,))
        degrees(0, (1,))
        keep_row(0, 1)
        factor_by_scalar(*units[1], range(PACK))

        degree_steps = {
            (0, (2,)): (1, 2, 3, 3),
            (0, (3,)): (2, 3, 4, 5),
            (1, (0, 1)): (10, 11, 11, 12),
            (1, (2, 3)): (14, 15, 15, 16),
        }
        regroups = {0: 0, 2: 1, 1: 1, 3: 2, 4: 4, 5: 6, 6: 8, 7: 10, 8: 12}
        AHEAD = 5
        waiting = []
        for index in range(2, len(units)):
            n, g = units[index]
            if kind(n, g) == "scalar" and chunks[n][1] % CHUNK == 0:
                waiting += [(index, *units[index], range(0, 2)), (index, *units[index], range(2, 4))]
        TAIL = 1
        starts = {}
        quantised = [0] * len(chunks)
        pairs = ((0, 1), (2, 3))
        banks = []
        for index, (n, g) in enumerate(units):
            if kind(n, g) != "scalar":
                banks += [(index, n, g, k) for k in range(max(1, chunks[n][2] // BANK_COLS))]

        def make_banks(step, limit):
            pending = len([1 for n, g in factors for bank in factors[(n, g)] if units.index((n, g)) > step and kind(n, g) != "scalar"])
            while banks and pending < limit:
                index, n, g, k = banks[0]
                b, c = chunks[n][0], chunks[n][1] // CHUNK
                if kind(n, g) == "mirror":
                    if (b, g, c) not in complete:
                        return
                elif (b, g) not in left_rows or (b, c) not in right_rows:
                    return
                factor_by_tensor(n, g, k)
                banks.remove(banks[0])
                pending += 1

        for step in range(len(units) + 14):
            for q, at in ((1, 7), (2, 8), (3, 12)):
                if step == at:
                    load_chunk(1, q)
            for key, at in degree_steps.items():
                if step == at[1]:
                    degrees(*key)
            for n, at in regroups.items():
                if step == at and (n == 2):
                    regroup_piece(n, nc.vector.tensor_copy)
            if step < len(units):
                scale(*units[step])
            for n, at in regroups.items():
                if step == at + 1 + (not (n == 2)):
                    quantise_piece(n)
                    if n + RAW_BUFS < len(pieces):
                        load_piece(n + RAW_BUFS)
            for lag in (3, 1):
                if 0 <= step - lag < len(units) and on_planes(*units[step - lag]) == (lag == 3):
                    n, g = units[step - lag]
                    quantise_a(n, g)
                    quantised[n] += 1
                    if quantised[n] == PASSES:
                        starts[n] = max(step + 1, starts[n - 1] + 3) if n > 0 else step + 1
            for n, at in starts.items():
                if step == at + 5:
                    quantise_h(n)
            for n, at in starts.items():
                if 0 <= step - at - 7 < chunks[n][2] // P:
                    store(n, step - at - 7)
            for n, at in starts.items():
                for pair in pairs:
                    if step == at + 1 + (pair[0] > 0 and n < last_chunk):
                        relu(n, pair)
                for half in range(chunks[n][2] // BANK_COLS):
                    if step == at + 3 + half:
                        regroup_h(n, half)
            for key, at in degree_steps.items():
                if step == at[2]:
                    for q in key[1]:
                        if key[0] == 0 or q == 0:
                            keep_row(key[0], q)
                    if key[0] == BATCH - 1:
                        split(*key)
                if step == at[3] and key[0] == BATCH - 1:
                    for q in key[1]:
                        turn(key[0], q)
            make_banks(step, 1)
            for n, at in starts.items():
                if 0 <= step - at - 6 < chunks[n][2] // P:
                    project(n, step - at - 6)
            make_banks(step, 2)
            for n, at in starts.items():
                if n < last_chunk and step == at:
                    aggregate(n, pairs[0], range(PASSES))
                if n < last_chunk and step == at:
                    aggregate(n, pairs[1], range(PASSES))
            if step >= len(units) - PASSES + 2 and step < len(units) + 2:
                g = step - (len(units) - PASSES + 2)
                for pair in pairs:
                    aggregate(last_chunk, pair, range(g, g + 1))
            make_banks(step, 3)
            for key, at in degree_steps.items():
                if step == at[0]:
                    column_sums(*key)
            if step < len(units) and on_planes(*units[step]):
                n, g = units[step]
                a_grouped[(n, g)] = regroup(nc.scalar.copy, a_planes[(n, g)], chunks[n][2])
            for n, at in regroups.items():
                if step == at and not (n == 2):
                    regroup_piece(n, nc.scalar.copy)
            emitted = 0
            for index, n, g, ts in waiting[:]:
                b, c = chunks[n][0], chunks[n][1] // CHUNK
                if (b, g) in d_col and (b, c) in d_row and (index <= step + 1 or (emitted == 0 and index <= step + AHEAD)):
                    factor_by_scalar(n, g, ts)
                    waiting.remove((index, n, g, ts))
                    emitted += 1
            if step == 4:
                turn_b2()
